import numpy as np
import ml_dtypes


def mxq(x, axis, fmt="e4m3"):
    dtype, down = {"e4m3": (ml_dtypes.float8_e4m3fn, 7), "e5m2": (ml_dtypes.float8_e5m2, 14)}[fmt]
    v = np.moveaxis(np.asarray(x, np.float32).astype(ml_dtypes.bfloat16).astype(np.float64), axis, -1)
    blocks = v.reshape(v.shape[:-1] + (-1, 32))
    amax = np.abs(blocks).max(-1, keepdims=True)
    byte = np.maximum(np.where(amax > 0, np.frexp(amax)[1] - 1 + 127, 0) - down, 1)
    scale = np.exp2(byte - 127.0)
    codes = (blocks / scale).astype(np.float32).astype(dtype).astype(np.float64)
    return np.moveaxis((codes * scale).reshape(v.shape), -1, axis)


WIDE = False


def mx_kscale(k):
    if not WIDE:
        return np.ones(k)
    levels = np.array([10, -10, 5, -5, 0])
    a = np.random.permutation(np.resize(levels, k // 512 * 4)).reshape(k // 512, 4)
    idx = np.arange(k)
    return np.exp2(a[idx // 512, idx % 128 // 32])


BF16 = ml_dtypes.bfloat16


def bf(x):
    return np.asarray(x, np.float32).astype(BF16)


def f64(x):
    return np.asarray(x).astype(np.float64)


B, P0, P1, P2, K0, K1, K2 = 128, 4096, 9216, 7168, 512, 512, 512
PT = P0 + P1 + P2
KT = K0 + K1 + K2
CLIP0 = 1.0


def clip_rows(mat, clip):
    norms = np.sqrt(np.sum(mat * mat, axis=1, keepdims=True))
    scale = np.minimum(clip / norms, 1.0)
    return mat * scale


def setup_inputs():
    s0, s1, s2 = mx_kscale(P0), mx_kscale(P1), mx_kscale(P2)
    r = np.exp2(np.random.uniform(-2.0, 2.0, (B, 1))) / (KT * PT) ** 0.25
    return {"target_grad": bf(np.random.standard_normal((B, PT)) * r * np.concatenate([s0, s1, s2])),
            "bases0": bf(np.random.standard_normal((P0, K0)) / np.sqrt(P0) / s0[:, None]),
            "bases1": bf(np.random.standard_normal((P1, K1)) / np.sqrt(P1) / s1[:, None]),
            "bases2": bf(np.random.standard_normal((P2, K2)) / np.sqrt(P2) / s2[:, None])}


def reference(target_grad, bases0, bases1, bases2):
    g = f64(target_grad)
    embeddings = []
    offset = 0
    for b in (f64(bases0), f64(bases1), f64(bases2)):
        num_p = b.shape[0]
        embeddings.append(mxq(g[:, offset:offset + num_p], 1, "e4m3") @ mxq(b, 0, "e4m3"))
        offset += num_p
    embedding = np.concatenate(embeddings, axis=1)
    avg_clipped_embedding = np.sum(clip_rows(embedding, CLIP0), axis=0) / B
    return embedding, avg_clipped_embedding

@@ -1,0 +1,174 @@
+from contextlib import ExitStack
+
+import concourse.mybir as mybir
+from concourse.masks import make_identity
+
+BF16 = mybir.dt.bfloat16
+F32 = mybir.dt.float32
+U32 = mybir.dt.uint32
+U8 = mybir.dt.uint8
+FP8X4 = mybir.dt.float8_e4m3fn_x4
+ACT = mybir.ActivationFunctionType
+ALU = mybir.AluOpType
+
+P = 128
+PACK = 4
+K_PASS = P * PACK
+CHUNK = 4
+BANK_PASSES = 2
+VECTOR_COLUMNS = 288
+CLIP = 1.0
+
+FLOPS = 2 * 128 * 20480 * 512 + 2 * 128 * 1536
+
+
+def tile_gep_pa_kernel(tc, target_grad, bases0, bases1, bases2, out_0, out_1):
+    nc = tc.nc
+    bases = (bases0, bases1, bases2)
+    n_groups = len(bases)
+    width = bases0.shape[1]
+
+    passes = []
+    for group, basis in enumerate(bases):
+        group_passes = basis.shape[0] // K_PASS
+        passes.extend((group, i, group_passes) for i in range(group_passes))
+    n_passes = len(passes)
+    n_chunks = n_passes // CHUNK
+    assert n_passes * K_PASS == target_grad.shape[1] and n_chunks * CHUNK == n_passes
+
+    with ExitStack() as ctx:
+        keep = ctx.enter_context(tc.tile_pool(name="keep", bufs=1))
+        grad_pool = ctx.enter_context(tc.tile_pool(name="grad", bufs=3))
+        raw_pool = ctx.enter_context(tc.tile_pool(name="raw", bufs=12))
+        work = ctx.enter_context(tc.tile_pool(name="work", bufs=3))
+        acc_pool = ctx.enter_context(tc.psum_pool(name="acc", bufs=1))
+        flip_pool = ctx.enter_context(tc.psum_pool(name="flip", bufs=3))
+        mean_pool = ctx.enter_context(tc.psum_pool(name="mean", bufs=2))
+        ctx.enter_context(tc.manual_schedule())
+
+        identity = keep.tile([P, P], F32, name="identity")
+        make_identity(nc, identity[:])
+
+        one = keep.tile([P, 1], F32, name="one")
+        nc.vector.memset(one[:], 1.0)
+        one_root = keep.tile([P, 1], F32, name="one_root")
+        nc.scalar.activation(out=one_root[:], in_=one[:], func=ACT.Sqrt)
+
+        grad_codes = keep.tile([P, n_passes * P], U32, name="grad_codes", align_bytes=64)
+        grad_scales = keep.tile([P, n_passes * P], U8, name="grad_scales", align_bytes=64)
+        sumsq = keep.tile([P, n_groups], F32, name="sumsq")
+        embedding = [keep.tile([P, width], F32, name="embedding%d" % g) for g in range(n_groups)]
+        acc = [acc_pool.tile([P, width], F32, name="acc%d" % g) for g in range(n_groups)]
+
+        flipped = {}
+        grad_grouped = {}
+
+        def transpose_grad(chunk):
+            columns = CHUNK * K_PASS
+            grad_raw = grad_pool.tile([P, columns], BF16, name="grad_raw")
+            nc.sync.dma_start(out=grad_raw[:], in_=target_grad[:, chunk * columns : (chunk + 1) * columns])
+            words = grad_raw[:].bitcast(F32).rearrange("b (c p u) -> b c u p", p=P, u=2)
+            flipped[chunk] = []
+            for first in range(0, CHUNK, BANK_PASSES):
+                bank = flip_pool.tile([P, BANK_PASSES, 2, P], F32, name="bank")
+                for c in range(BANK_PASSES):
+                    for u in range(2):
+                        nc.tensor.transpose(bank[:, c, u, :], words[:, first + c, u, :], identity[:])
+                flipped[chunk].append(bank)
+
+        def copy_grad(chunk):
+            grad_grouped[chunk] = grad_pool.tile([P, CHUNK * P * PACK], BF16, name="grad_grouped", align_bytes=64)
+            grouped_words = grad_grouped[chunk][:].bitcast(F32).rearrange("p (c b u) -> p c b u", b=P, u=2)
+            for n, bank in enumerate(flipped[chunk]):
+                nc.scalar.copy(
+                    out=grouped_words[:, n * BANK_PASSES : (n + 1) * BANK_PASSES],
+                    in_=bank[:].rearrange("p c u b -> p c b u"),
+                )
+
+        def quantise_grad(chunk):
+            cols = slice(chunk * CHUNK * P, (chunk + 1) * CHUNK * P)
+            nc.vector.quantize_mx(
+                out=grad_codes[:, cols].bitcast(FP8X4), scales=grad_scales[:, cols], in_=grad_grouped[chunk][:]
+            )
+
+        grouped = {}
+
+        def regroup_basis(c):
+            group, i, group_passes = passes[c]
+            raw = raw_pool.tile([P, PACK, width], BF16, name="raw")
+            rows = bases[group][i * K_PASS : (i + 1) * K_PASS, :]
+            nc.sync.dma_start(out=raw[:], in_=rows.rearrange("(p j) n -> p j n", j=PACK))
+            grouped[c] = work.tile([P, width, PACK], BF16, name="grouped", align_bytes=64)
+            nc.vector.tensor_copy(
+                out=grouped[c][:, :VECTOR_COLUMNS, :].rearrange("p (c i) j -> p c j i", i=4),
+                in_=raw[:, :, :VECTOR_COLUMNS].rearrange("p j (c i) -> p c j i", i=4),
+            )
+            nc.scalar.copy(
+                out=grouped[c][:, VECTOR_COLUMNS:, :].rearrange("p (c i) j -> p c j i", i=4),
+                in_=raw[:, :, VECTOR_COLUMNS:].rearrange("p j (c i) -> p c j i", i=4),
+            )
+
+        def multiply(c):
+            group, i, group_passes = passes[c]
+            codes = work.tile([P, width], U32, name="codes", align_bytes=64)
+            scales = work.tile([P, width], U8, name="scales", align_bytes=64)
+            nc.vector.quantize_mx(
+                out=codes[:].bitcast(FP8X4), scales=scales[:], in_=grouped[c][:].rearrange("p n j -> p (n j)")
+            )
+            nc.tensor.matmul_mx(
+                out=acc[group][:],
+                lhsT=grad_codes[:, c * P : (c + 1) * P].bitcast(FP8X4),
+                lhsT_scale=grad_scales[:, c * P : (c + 1) * P],
+                rhs=codes[:].bitcast(FP8X4),
+                rhs_scale=scales[:],
+                start=(i == 0),
+                stop=(i == group_passes - 1),
+            )
+
+        def sum_squares(group):
+            squares = work.tile([P, width], F32, name="squares")
+            nc.scalar.activation(
+                out=squares[:], in_=acc[group][:], func=ACT.Square, accum_out=sumsq[:, group : group + 1]
+            )
+
+        def store_embedding(group):
+            nc.scalar.copy(out=embedding[group][:], in_=acc[group][:])
+            nc.scalar.dma_start(out=out_0[:, group * width : (group + 1) * width], in_=embedding[group][:])
+
+        for c in range(-6, n_passes + 1):
+            if c % CHUNK == 0 and 0 <= (c + 4) // CHUNK < n_chunks:
+                copy_grad((c + 4) // CHUNK)
+            if 0 <= c < n_passes:
+                regroup_basis(c)
+            if c % CHUNK == 2 and 0 <= (c + 2) // CHUNK < n_chunks:
+                quantise_grad((c + 2) // CHUNK)
+            if c % CHUNK == 2 and 0 <= (c + 6) // CHUNK < n_chunks:
+                transpose_grad((c + 6) // CHUNK)
+            if c >= 1:
+                multiply(c - 1)
+            if c >= 2 and passes[c - 2][1] == passes[c - 2][2] - 1:
+                sum_squares(passes[c - 2][0])
+                store_embedding(passes[c - 2][0])
+
+        last = n_groups - 1
+        early = keep.tile([P, 1], F32, name="early")
+        nc.vector.tensor_reduce(out=early[:], in_=sumsq[:, :last], op=ALU.add, axis=mybir.AxisListType.X)
+        sum_squares(last)
+        norm = keep.tile([P, 1], F32, name="norm")
+        nc.scalar.activation(out=norm[:], in_=sumsq[:, last : last + 1], func=ACT.Sqrt, bias=early[:])
+        store_embedding(last)
+        inverse = keep.tile([P, 1], F32, name="inverse")
+        nc.vector.reciprocal(out=inverse[:], in_=norm[:])
+        factor = keep.tile([P, 1], F32, name="factor")
+        nc.vector.tensor_scalar(
+            out=factor[:], in0=inverse[:], scalar1=CLIP / P, scalar2=1.0 / P, op0=ALU.mult, op1=ALU.min
+        )
+
+        mean = keep.tile([P, n_groups * width], F32, name="mean")
+        for group in range(n_groups):
+            mean_acc = mean_pool.tile([P, width], F32, name="mean_acc")
+            nc.tensor.matmul(
+                out=mean_acc[:], lhsT=factor[:, 0:1].to_broadcast([P, P]), rhs=embedding[group][:], start=True, stop=True
+            )
+            nc.vector.tensor_copy(out=mean[:, group * width : (group + 1) * width], in_=mean_acc[:])
+        nc.sync.dma_start(out=out_1.rearrange("(o n) -> o n", o=1), in_=mean[0:1, :])

@@ -14,9 +14,8 @@ ALU = mybir.AluOpType
 P = 128
 PACK = 4
 K_PASS = P * PACK
-CHUNK = 4
-BANK_PASSES = 2
-VECTOR_COLUMNS = 288
+PAIR = 2
+CHUNK = 2
 CLIP = 1.0
 
 FLOPS = 2 * 128 * 20480 * 512 + 2 * 128 * 1536
@@ -32,14 +31,14 @@ def tile_gep_pa_kernel(tc, target_grad, bases0, bases1, bases2, out_0, out_1):
     for group, basis in enumerate(bases):
         group_passes = basis.shape[0] // K_PASS
         passes.extend((group, i, group_passes) for i in range(group_passes))
-    n_passes = len(passes)
-    n_chunks = n_passes // CHUNK
-    assert n_passes * K_PASS == target_grad.shape[1] and n_chunks * CHUNK == n_passes
+    n_pairs = len(passes) // PAIR
+    n_chunks = n_pairs // CHUNK
+    assert len(passes) * K_PASS == target_grad.shape[1] and n_chunks * CHUNK * PAIR == len(passes)
 
     with ExitStack() as ctx:
         keep = ctx.enter_context(tc.tile_pool(name="keep", bufs=1))
         grad_pool = ctx.enter_context(tc.tile_pool(name="grad", bufs=3))
-        raw_pool = ctx.enter_context(tc.tile_pool(name="raw", bufs=12))
+        raw_pool = ctx.enter_context(tc.tile_pool(name="raw", bufs=6))
         work = ctx.enter_context(tc.tile_pool(name="work", bufs=3))
         acc_pool = ctx.enter_context(tc.psum_pool(name="acc", bufs=1))
         flip_pool = ctx.enter_context(tc.psum_pool(name="flip", bufs=3))
@@ -54,8 +53,8 @@ def tile_gep_pa_kernel(tc, target_grad, bases0, bases1, bases2, out_0, out_1):
         one_root = keep.tile([P, 1], F32, name="one_root")
         nc.scalar.activation(out=one_root[:], in_=one[:], func=ACT.Sqrt)
 
-        grad_codes = keep.tile([P, n_passes * P], U32, name="grad_codes", align_bytes=64)
-        grad_scales = keep.tile([P, n_passes * P], U8, name="grad_scales", align_bytes=64)
+        grad_codes = keep.tile([P, len(passes) * P], U32, name="grad_codes", align_bytes=64)
+        grad_scales = keep.tile([P, len(passes) * P], U8, name="grad_scales", align_bytes=64)
         sumsq = keep.tile([P, n_groups], F32, name="sumsq")
         embedding = [keep.tile([P, width], F32, name="embedding%d" % g) for g in range(n_groups)]
         acc = [acc_pool.tile([P, width], F32, name="acc%d" % g) for g in range(n_groups)]
@@ -64,66 +63,67 @@ def tile_gep_pa_kernel(tc, target_grad, bases0, bases1, bases2, out_0, out_1):
         grad_grouped = {}
 
         def transpose_grad(chunk):
-            columns = CHUNK * K_PASS
+            columns = CHUNK * PAIR * K_PASS
             grad_raw = grad_pool.tile([P, columns], BF16, name="grad_raw")
             nc.sync.dma_start(out=grad_raw[:], in_=target_grad[:, chunk * columns : (chunk + 1) * columns])
             words = grad_raw[:].bitcast(F32).rearrange("b (c p u) -> b c u p", p=P, u=2)
             flipped[chunk] = []
-            for first in range(0, CHUNK, BANK_PASSES):
-                bank = flip_pool.tile([P, BANK_PASSES, 2, P], F32, name="bank")
-                for c in range(BANK_PASSES):
+            for pair in range(CHUNK):
+                bank = flip_pool.tile([P, PAIR, 2, P], F32, name="bank")
+                for c in range(PAIR):
                     for u in range(2):
-                        nc.tensor.transpose(bank[:, c, u, :], words[:, first + c, u, :], identity[:])
+                        nc.tensor.transpose(bank[:, c, u, :], words[:, pair * PAIR + c, u, :], identity[:])
                 flipped[chunk].append(bank)
 
         def copy_grad(chunk):
-            grad_grouped[chunk] = grad_pool.tile([P, CHUNK * P * PACK], BF16, name="grad_grouped", align_bytes=64)
+            grad_grouped[chunk] = grad_pool.tile(
+                [P, CHUNK * PAIR * P * PACK], BF16, name="grad_grouped", align_bytes=64
+            )
             grouped_words = grad_grouped[chunk][:].bitcast(F32).rearrange("p (c b u) -> p c b u", b=P, u=2)
-            for n, bank in enumerate(flipped[chunk]):
+            for pair, bank in enumerate(flipped[chunk]):
                 nc.scalar.copy(
-                    out=grouped_words[:, n * BANK_PASSES : (n + 1) * BANK_PASSES],
+                    out=grouped_words[:, pair * PAIR : (pair + 1) * PAIR],
                     in_=bank[:].rearrange("p c u b -> p c b u"),
                 )
 
         def quantise_grad(chunk):
-            cols = slice(chunk * CHUNK * P, (chunk + 1) * CHUNK * P)
+            cols = slice(chunk * CHUNK * PAIR * P, (chunk + 1) * CHUNK * PAIR * P)
             nc.vector.quantize_mx(
                 out=grad_codes[:, cols].bitcast(FP8X4), scales=grad_scales[:, cols], in_=grad_grouped[chunk][:]
             )
 
         grouped = {}
 
-        def regroup_basis(c):
-            group, i, group_passes = passes[c]
-            raw = raw_pool.tile([P, PACK, width], BF16, name="raw")
-            rows = bases[group][i * K_PASS : (i + 1) * K_PASS, :]
-            nc.sync.dma_start(out=raw[:], in_=rows.rearrange("(p j) n -> p j n", j=PACK))
-            grouped[c] = work.tile([P, width, PACK], BF16, name="grouped", align_bytes=64)
-            nc.vector.tensor_copy(
-                out=grouped[c][:, :VECTOR_COLUMNS, :].rearrange("p (c i) j -> p c j i", i=4),
-                in_=raw[:, :, :VECTOR_COLUMNS].rearrange("p j (c i) -> p c j i", i=4),
-            )
-            nc.scalar.copy(
-                out=grouped[c][:, VECTOR_COLUMNS:, :].rearrange("p (c i) j -> p c j i", i=4),
-                in_=raw[:, :, VECTOR_COLUMNS:].rearrange("p j (c i) -> p c j i", i=4),
-            )
+        def regroup_basis(q):
+            grouped[q] = work.tile([P, PAIR, width, PACK], BF16, name="grouped", align_bytes=64)
+            for half, copy in enumerate((nc.scalar.copy, nc.vector.tensor_copy)):
+                group, i, group_passes = passes[q * PAIR + half]
+                raw = raw_pool.tile([P, PACK, width], BF16, name="raw%d" % half)
+                rows = bases[group][i * K_PASS : (i + 1) * K_PASS, :]
+                nc.sync.dma_start(out=raw[:], in_=rows.rearrange("(p j) n -> p j n", j=PACK))
+                copy(
+                    out=grouped[q][:, half].rearrange("p (c i) j -> p c j i", i=4),
+                    in_=raw[:].rearrange("p j (c i) -> p c j i", i=4),
+                )
 
-        def multiply(c):
-            group, i, group_passes = passes[c]
-            codes = work.tile([P, width], U32, name="codes", align_bytes=64)
-            scales = work.tile([P, width], U8, name="scales", align_bytes=64)
+        def multiply(q):
+            codes = work.tile([P, PAIR * width], U32, name="codes", align_bytes=64)
+            scales = work.tile([P, PAIR * width], U8, name="scales", align_bytes=64)
             nc.vector.quantize_mx(
-                out=codes[:].bitcast(FP8X4), scales=scales[:], in_=grouped[c][:].rearrange("p n j -> p (n j)")
+                out=codes[:].bitcast(FP8X4), scales=scales[:], in_=grouped[q][:].rearrange("p h n j -> p (h n j)")
             )
-            nc.tensor.matmul_mx(
-                out=acc[group][:],
-                lhsT=grad_codes[:, c * P : (c + 1) * P].bitcast(FP8X4),
-                lhsT_scale=grad_scales[:, c * P : (c + 1) * P],
-                rhs=codes[:].bitcast(FP8X4),
-                rhs_scale=scales[:],
-                start=(i == 0),
-                stop=(i == group_passes - 1),
-            )
+            for half in range(PAIR):
+                c = q * PAIR + half
+                group, i, group_passes = passes[c]
+                nc.tensor.matmul_mx(
+                    out=acc[group][:],
+                    lhsT=grad_codes[:, c * P : (c + 1) * P].bitcast(FP8X4),
+                    lhsT_scale=grad_scales[:, c * P : (c + 1) * P],
+                    rhs=codes[:, half * width : (half + 1) * width].bitcast(FP8X4),
+                    rhs_scale=scales[:, half * width : (half + 1) * width],
+                    start=(i == 0),
+                    stop=(i == group_passes - 1),
+                )
 
         def sum_squares(group):
             squares = work.tile([P, width], F32, name="squares")
@@ -135,20 +135,22 @@ def tile_gep_pa_kernel(tc, target_grad, bases0, bases1, bases2, out_0, out_1):
             nc.scalar.copy(out=embedding[group][:], in_=acc[group][:])
             nc.scalar.dma_start(out=out_0[:, group * width : (group + 1) * width], in_=embedding[group][:])
 
-        for c in range(-6, n_passes + 1):
-            if c % CHUNK == 0 and 0 <= (c + 4) // CHUNK < n_chunks:
-                copy_grad((c + 4) // CHUNK)
-            if 0 <= c < n_passes:
-                regroup_basis(c)
-            if c % CHUNK == 2 and 0 <= (c + 2) // CHUNK < n_chunks:
-                quantise_grad((c + 2) // CHUNK)
-            if c % CHUNK == 2 and 0 <= (c + 6) // CHUNK < n_chunks:
-                transpose_grad((c + 6) // CHUNK)
-            if c >= 1:
-                multiply(c - 1)
-            if c >= 2 and passes[c - 2][1] == passes[c - 2][2] - 1:
-                sum_squares(passes[c - 2][0])
-                store_embedding(passes[c - 2][0])
+        for q in range(-2, n_pairs + 1):
+            if q % CHUNK == 1 and 0 <= (q + 1) // CHUNK < n_chunks:
+                copy_grad((q + 1) // CHUNK)
+            if 0 <= q < n_pairs:
+                regroup_basis(q)
+            if q % CHUNK == 0 and 0 <= q // CHUNK < n_chunks:
+                quantise_grad(q // CHUNK)
+            if q % CHUNK == 0 and 0 <= (q + 2) // CHUNK < n_chunks:
+                transpose_grad((q + 2) // CHUNK)
+            if q >= 1:
+                multiply(q - 1)
+            if q >= 2:
+                group, i, group_passes = passes[(q - 2) * PAIR + 1]
+                if i == group_passes - 1:
+                    sum_squares(group)
+                    store_embedding(group)
 
         last = n_groups - 1
         early = keep.tile([P, 1], F32, name="early")

@@ -42,7 +42,7 @@ def tile_gep_pa_kernel(tc, target_grad, bases0, bases1, bases2, out_0, out_1):
         work = ctx.enter_context(tc.tile_pool(name="work", bufs=3))
         acc_pool = ctx.enter_context(tc.psum_pool(name="acc", bufs=1))
         flip_pool = ctx.enter_context(tc.psum_pool(name="flip", bufs=3))
-        mean_pool = ctx.enter_context(tc.psum_pool(name="mean", bufs=2))
+        mean_pool = ctx.enter_context(tc.psum_pool(name="mean", bufs=1))
         ctx.enter_context(tc.manual_schedule())
 
         identity = keep.tile([P, P], F32, name="identity")
@@ -52,6 +52,9 @@ def tile_gep_pa_kernel(tc, target_grad, bases0, bases1, bases2, out_0, out_1):
         nc.vector.memset(one[:], 1.0)
         one_root = keep.tile([P, 1], F32, name="one_root")
         nc.scalar.activation(out=one_root[:], in_=one[:], func=ACT.Sqrt)
+
+        mean_upright = keep.tile([P, P], F32, name="mean_upright")
+        nc.gpsimd.memset(mean_upright[:], 0.0)
 
         grad_codes = keep.tile([P, len(passes) * P], U32, name="grad_codes", align_bytes=64)
         grad_scales = keep.tile([P, len(passes) * P], U8, name="grad_scales", align_bytes=64)
@@ -166,11 +169,20 @@ def tile_gep_pa_kernel(tc, target_grad, bases0, bases1, bases2, out_0, out_1):
             out=factor[:], in0=inverse[:], scalar1=CLIP / P, scalar2=1.0 / P, op0=ALU.mult, op1=ALU.min
         )
 
-        mean = keep.tile([P, n_groups * width], F32, name="mean")
-        for group in range(n_groups):
-            mean_acc = mean_pool.tile([P, width], F32, name="mean_acc")
+        blocks = n_groups * width // P
+        mean_upright_acc = mean_pool.tile([P, blocks], F32, name="mean_upright_acc")
+        for block in range(blocks):
+            group, part = divmod(block, width // P)
             nc.tensor.matmul(
-                out=mean_acc[:], lhsT=factor[:, 0:1].to_broadcast([P, P]), rhs=embedding[group][:], start=True, stop=True
+                out=mean_upright_acc[:, block : block + 1],
+                lhsT=embedding[group][:, part * P : (part + 1) * P],
+                rhs=factor[:],
+                start=True,
+                stop=True,
             )
-            nc.vector.tensor_copy(out=mean[:, group * width : (group + 1) * width], in_=mean_acc[:])
-        nc.sync.dma_start(out=out_1.rearrange("(o n) -> o n", o=1), in_=mean[0:1, :])
+        nc.vector.tensor_copy(out=mean_upright[:, :blocks], in_=mean_upright_acc[:])
+        mean_acc = mean_pool.tile([P, P], F32, name="mean_acc")
+        nc.tensor.transpose(mean_acc[:], mean_upright[:], identity[:])
+        mean = keep.tile([P, P], F32, name="mean")
+        nc.vector.tensor_copy(out=mean[:], in_=mean_acc[:])
+        nc.sync.dma_start(out=out_1.rearrange("(r n) -> r n", n=P), in_=mean[:blocks, :])

@@ -39,10 +39,9 @@ def tile_gep_pa_kernel(tc, target_grad, bases0, bases1, bases2, out_0, out_1):
         keep = ctx.enter_context(tc.tile_pool(name="keep", bufs=1))
         grad_pool = ctx.enter_context(tc.tile_pool(name="grad", bufs=3))
         raw_pool = ctx.enter_context(tc.tile_pool(name="raw", bufs=6))
-        work = ctx.enter_context(tc.tile_pool(name="work", bufs=3))
+        work = ctx.enter_context(tc.tile_pool(name="work", bufs=4))
         acc_pool = ctx.enter_context(tc.psum_pool(name="acc", bufs=1))
-        flip_pool = ctx.enter_context(tc.psum_pool(name="flip", bufs=3))
-        mean_pool = ctx.enter_context(tc.psum_pool(name="mean", bufs=1))
+        bank_pool = ctx.enter_context(tc.psum_pool(name="bank", bufs=5))
         ctx.enter_context(tc.manual_schedule())
 
         identity = keep.tile([P, P], F32, name="identity")
@@ -52,9 +51,6 @@ def tile_gep_pa_kernel(tc, target_grad, bases0, bases1, bases2, out_0, out_1):
         nc.vector.memset(one[:], 1.0)
         one_root = keep.tile([P, 1], F32, name="one_root")
         nc.scalar.activation(out=one_root[:], in_=one[:], func=ACT.Sqrt)
-
-        mean_upright = keep.tile([P, P], F32, name="mean_upright")
-        nc.gpsimd.memset(mean_upright[:], 0.0)
 
         grad_codes = keep.tile([P, len(passes) * P], U32, name="grad_codes", align_bytes=64)
         grad_scales = keep.tile([P, len(passes) * P], U8, name="grad_scales", align_bytes=64)
@@ -72,7 +68,7 @@ def tile_gep_pa_kernel(tc, target_grad, bases0, bases1, bases2, out_0, out_1):
             words = grad_raw[:].bitcast(F32).rearrange("b (c p u) -> b c u p", p=P, u=2)
             flipped[chunk] = []
             for pair in range(CHUNK):
-                bank = flip_pool.tile([P, PAIR, 2, P], F32, name="bank")
+                bank = bank_pool.tile([P, PAIR, 2, P], F32, name="bank")
                 for c in range(PAIR):
                     for u in range(2):
                         nc.tensor.transpose(bank[:, c, u, :], words[:, pair * PAIR + c, u, :], identity[:])
@@ -95,38 +91,37 @@ def tile_gep_pa_kernel(tc, target_grad, bases0, bases1, bases2, out_0, out_1):
                 out=grad_codes[:, cols].bitcast(FP8X4), scales=grad_scales[:, cols], in_=grad_grouped[chunk][:]
             )
 
-        grouped = {}
+        def load_basis(c, half):
+            group, i, group_passes = passes[c]
+            raw = raw_pool.tile([P, PACK, width], BF16, name="raw%d" % half)
+            rows = bases[group][i * K_PASS : (i + 1) * K_PASS, :]
+            nc.sync.dma_start(out=raw[:], in_=rows.rearrange("(p j) n -> p j n", j=PACK))
+            return raw
 
-        def regroup_basis(q):
-            grouped[q] = work.tile([P, PAIR, width, PACK], BF16, name="grouped", align_bytes=64)
-            for half, copy in enumerate((nc.scalar.copy, nc.vector.tensor_copy)):
-                group, i, group_passes = passes[q * PAIR + half]
-                raw = raw_pool.tile([P, PACK, width], BF16, name="raw%d" % half)
-                rows = bases[group][i * K_PASS : (i + 1) * K_PASS, :]
-                nc.sync.dma_start(out=raw[:], in_=rows.rearrange("(p j) n -> p j n", j=PACK))
-                copy(
-                    out=grouped[q][:, half].rearrange("p (c i) j -> p c j i", i=4),
-                    in_=raw[:].rearrange("p j (c i) -> p c j i", i=4),
-                )
-
-        def multiply(q):
-            codes = work.tile([P, PAIR * width], U32, name="codes", align_bytes=64)
-            scales = work.tile([P, PAIR * width], U8, name="scales", align_bytes=64)
-            nc.vector.quantize_mx(
-                out=codes[:].bitcast(FP8X4), scales=scales[:], in_=grouped[q][:].rearrange("p h n j -> p (h n j)")
+        def regroup(copy, raw, half):
+            grouped = work.tile([P, width, PACK], BF16, name="grouped%d" % half, align_bytes=64)
+            copy(
+                out=grouped[:].rearrange("p (c i) j -> p c j i", i=4),
+                in_=raw[:].rearrange("p j (c i) -> p c j i", i=4),
             )
-            for half in range(PAIR):
-                c = q * PAIR + half
-                group, i, group_passes = passes[c]
-                nc.tensor.matmul_mx(
-                    out=acc[group][:],
-                    lhsT=grad_codes[:, c * P : (c + 1) * P].bitcast(FP8X4),
-                    lhsT_scale=grad_scales[:, c * P : (c + 1) * P],
-                    rhs=codes[:, half * width : (half + 1) * width].bitcast(FP8X4),
-                    rhs_scale=scales[:, half * width : (half + 1) * width],
-                    start=(i == 0),
-                    stop=(i == group_passes - 1),
-                )
+            return grouped
+
+        def multiply(c, grouped):
+            group, i, group_passes = passes[c]
+            codes = work.tile([P, width], U32, name="codes", align_bytes=64)
+            scales = work.tile([P, width], U8, name="scales", align_bytes=64)
+            nc.vector.quantize_mx(
+                out=codes[:].bitcast(FP8X4), scales=scales[:], in_=grouped[:].rearrange("p n j -> p (n j)")
+            )
+            nc.tensor.matmul_mx(
+                out=acc[group][:],
+                lhsT=grad_codes[:, c * P : (c + 1) * P].bitcast(FP8X4),
+                lhsT_scale=grad_scales[:, c * P : (c + 1) * P],
+                rhs=codes[:].bitcast(FP8X4),
+                rhs_scale=scales[:],
+                start=(i == 0),
+                stop=(i == group_passes - 1),
+            )
 
         def sum_squares(group):
             squares = work.tile([P, width], F32, name="squares")
@@ -134,55 +129,55 @@ def tile_gep_pa_kernel(tc, target_grad, bases0, bases1, bases2, out_0, out_1):
                 out=squares[:], in_=acc[group][:], func=ACT.Square, accum_out=sumsq[:, group : group + 1]
             )
 
-        def store_embedding(group):
-            nc.scalar.copy(out=embedding[group][:], in_=acc[group][:])
-            nc.scalar.dma_start(out=out_0[:, group * width : (group + 1) * width], in_=embedding[group][:])
+        def copy_embedding(group):
+            nc.vector.tensor_copy(out=embedding[group][:], in_=acc[group][:])
 
-        for q in range(-2, n_pairs + 1):
-            if q % CHUNK == 1 and 0 <= (q + 1) // CHUNK < n_chunks:
-                copy_grad((q + 1) // CHUNK)
-            if 0 <= q < n_pairs:
-                regroup_basis(q)
-            if q % CHUNK == 0 and 0 <= q // CHUNK < n_chunks:
-                quantise_grad(q // CHUNK)
-            if q % CHUNK == 0 and 0 <= (q + 2) // CHUNK < n_chunks:
-                transpose_grad((q + 2) // CHUNK)
-            if q >= 1:
-                multiply(q - 1)
-            if q >= 2:
-                group, i, group_passes = passes[(q - 2) * PAIR + 1]
-                if i == group_passes - 1:
-                    sum_squares(group)
-                    store_embedding(group)
+        def store_embedding(group):
+            nc.sync.dma_start(out=out_0[:, group * width : (group + 1) * width], in_=embedding[group][:])
 
         last = n_groups - 1
+        for q in range(-4, n_pairs):
+            if q >= 0:
+                raw_first = load_basis(q * PAIR, 0)
+                raw_second = load_basis(q * PAIR + 1, 1)
+                grouped_first = regroup(nc.scalar.copy, raw_first, 0)
+                grouped_second = regroup(nc.vector.tensor_copy, raw_second, 1)
+                multiply(q * PAIR, grouped_first)
+                multiply(q * PAIR + 1, grouped_second)
+            if q % CHUNK == 1 and 0 <= (q + 1) // CHUNK < n_chunks:
+                quantise_grad((q + 1) // CHUNK)
+            if q % CHUNK == 0 and 0 <= (q + 2) // CHUNK < n_chunks:
+                copy_grad((q + 2) // CHUNK)
+            if q % CHUNK == 0 and 0 <= (q + 4) // CHUNK < n_chunks:
+                transpose_grad((q + 4) // CHUNK)
+            if q >= 1:
+                group, i, group_passes = passes[q * PAIR - 1]
+                if i == group_passes - 1:
+                    sum_squares(group)
+                    copy_embedding(group)
+
+        for group in range(last):
+            store_embedding(group)
+
         early = keep.tile([P, 1], F32, name="early")
         nc.vector.tensor_reduce(out=early[:], in_=sumsq[:, :last], op=ALU.add, axis=mybir.AxisListType.X)
         sum_squares(last)
         norm = keep.tile([P, 1], F32, name="norm")
         nc.scalar.activation(out=norm[:], in_=sumsq[:, last : last + 1], func=ACT.Sqrt, bias=early[:])
-        store_embedding(last)
         inverse = keep.tile([P, 1], F32, name="inverse")
         nc.vector.reciprocal(out=inverse[:], in_=norm[:])
         factor = keep.tile([P, 1], F32, name="factor")
         nc.vector.tensor_scalar(
             out=factor[:], in0=inverse[:], scalar1=CLIP / P, scalar2=1.0 / P, op0=ALU.mult, op1=ALU.min
         )
+        copy_embedding(last)
+        store_embedding(last)
 
-        blocks = n_groups * width // P
-        mean_upright_acc = mean_pool.tile([P, blocks], F32, name="mean_upright_acc")
-        for block in range(blocks):
-            group, part = divmod(block, width // P)
+        mean = keep.tile([P, n_groups * width], F32, name="mean")
+        for group in range(n_groups):
+            mean_acc = bank_pool.tile([P, width], F32, name="mean_acc", tag="bank")
             nc.tensor.matmul(
-                out=mean_upright_acc[:, block : block + 1],
-                lhsT=embedding[group][:, part * P : (part + 1) * P],
-                rhs=factor[:],
-                start=True,
-                stop=True,
+                out=mean_acc[:], lhsT=factor[:, 0:1].to_broadcast([P, P]), rhs=embedding[group][:], start=True, stop=True
             )
-        nc.vector.tensor_copy(out=mean_upright[:, :blocks], in_=mean_upright_acc[:])
-        mean_acc = mean_pool.tile([P, P], F32, name="mean_acc")
-        nc.tensor.transpose(mean_acc[:], mean_upright[:], identity[:])
-        mean = keep.tile([P, P], F32, name="mean")
-        nc.vector.tensor_copy(out=mean[:], in_=mean_acc[:])
-        nc.sync.dma_start(out=out_1.rearrange("(r n) -> r n", n=P), in_=mean[:blocks, :])
+            nc.vector.tensor_copy(out=mean[:, group * width : (group + 1) * width], in_=mean_acc[:])
+        nc.sync.dma_start(out=out_1.rearrange("(o n) -> o n", o=1), in_=mean[0:1, :])

@@ -101,8 +101,8 @@ def tile_gep_pa_kernel(tc, target_grad, bases0, bases1, bases2, out_0, out_1):
         def regroup(copy, raw, half):
             grouped = work.tile([P, width, PACK], BF16, name="grouped%d" % half, align_bytes=64)
             copy(
-                out=grouped[:].rearrange("p (c i) j -> p c j i", i=4),
-                in_=raw[:].rearrange("p j (c i) -> p c j i", i=4),
+                out=grouped[:].rearrange("p (c i) j -> p c j i", i=8),
+                in_=raw[:].rearrange("p j (c i) -> p c j i", i=8),
             )
             return grouped
 

@@ -50,7 +50,10 @@ def tile_gep_pa_kernel(tc, target_grad, bases0, bases1, bases2, out_0, out_1):
         one = keep.tile([P, 1], F32, name="one")
         nc.vector.memset(one[:], 1.0)
         one_root = keep.tile([P, 1], F32, name="one_root")
-        nc.scalar.activation(out=one_root[:], in_=one[:], func=ACT.Sqrt)
+        nc.scalar.activation(out=one_root[:], in_=one[:], func=ACT.Abs_reciprocal_sqrt)
+
+        zeros = keep.tile([P, width], BF16, name="zeros")
+        nc.gpsimd.memset(zeros[:], 0.0)
 
         grad_codes = keep.tile([P, len(passes) * P], U32, name="grad_codes", align_bytes=64)
         grad_scales = keep.tile([P, len(passes) * P], U8, name="grad_scales", align_bytes=64)
@@ -123,6 +126,11 @@ def tile_gep_pa_kernel(tc, target_grad, bases0, bases1, bases2, out_0, out_1):
                 stop=(i == group_passes - 1),
             )
 
+        def keep_clock(count):
+            idle_acc = bank_pool.tile([P, width], F32, name="idle_acc", tag="bank")
+            for unused in range(count):
+                nc.tensor.matmul(out=idle_acc[:], lhsT=zeros[:, :P], rhs=zeros[:], start=True, stop=True)
+
         def sum_squares(group):
             squares = work.tile([P, width], F32, name="squares")
             nc.scalar.activation(
@@ -155,6 +163,8 @@ def tile_gep_pa_kernel(tc, target_grad, bases0, bases1, bases2, out_0, out_1):
                 if i == group_passes - 1:
                     sum_squares(group)
                     copy_embedding(group)
+            if q == n_pairs - 2:
+                keep_clock(2)
 
         for group in range(last):
             store_embedding(group)
@@ -162,10 +172,11 @@ def tile_gep_pa_kernel(tc, target_grad, bases0, bases1, bases2, out_0, out_1):
         early = keep.tile([P, 1], F32, name="early")
         nc.vector.tensor_reduce(out=early[:], in_=sumsq[:, :last], op=ALU.add, axis=mybir.AxisListType.X)
         sum_squares(last)
-        norm = keep.tile([P, 1], F32, name="norm")
-        nc.scalar.activation(out=norm[:], in_=sumsq[:, last : last + 1], func=ACT.Sqrt, bias=early[:])
+        keep_clock(3)
         inverse = keep.tile([P, 1], F32, name="inverse")
-        nc.vector.reciprocal(out=inverse[:], in_=norm[:])
+        nc.scalar.activation(
+            out=inverse[:], in_=sumsq[:, last : last + 1], func=ACT.Abs_reciprocal_sqrt, bias=early[:]
+        )
         factor = keep.tile([P, 1], F32, name="factor")
         nc.vector.tensor_scalar(
             out=factor[:], in0=inverse[:], scalar1=CLIP / P, scalar2=1.0 / P, op0=ALU.mult, op1=ALU.min
@@ -174,10 +185,17 @@ def tile_gep_pa_kernel(tc, target_grad, bases0, bases1, bases2, out_0, out_1):
         store_embedding(last)
 
         mean = keep.tile([P, n_groups * width], F32, name="mean")
-        for group in range(n_groups):
+        half = width // 2
+        parts = [(group, 0, width) for group in range(last)] + [(last, 0, half), (last, half, width)]
+        for index, (group, begin, end) in enumerate(parts):
             mean_acc = bank_pool.tile([P, width], F32, name="mean_acc", tag="bank")
             nc.tensor.matmul(
-                out=mean_acc[:], lhsT=factor[:, 0:1].to_broadcast([P, P]), rhs=embedding[group][:], start=True, stop=True
+                out=mean_acc[:, : end - begin],
+                lhsT=factor[:, 0:1].to_broadcast([P, P]),
+                rhs=embedding[group][:, begin:end],
+                start=True,
+                stop=True,
             )
-            nc.vector.tensor_copy(out=mean[:, group * width : (group + 1) * width], in_=mean_acc[:])
+            copy = nc.scalar.copy if index % 2 else nc.vector.tensor_copy
+            copy(out=mean[:, group * width + begin : group * width + end], in_=mean_acc[:, : end - begin])
         nc.sync.dma_start(out=out_1.rearrange("(o n) -> o n", o=1), in_=mean[0:1, :])

@@ -15,7 +15,10 @@ P = 128
 PACK = 4
 K_PASS = P * PACK
 PAIR = 2
-CHUNK = 2
+LINE = 8
+SCALAR_COLS = 240
+AHEAD = 6
+GRAD_DELAY = 2
 CLIP = 1.0
 
 FLOPS = 2 * 128 * 20480 * 512 + 2 * 128 * 1536
@@ -30,16 +33,21 @@ def tile_gep_pa_kernel(tc, target_grad, bases0, bases1, bases2, out_0, out_1):
     passes = []
     for group, basis in enumerate(bases):
         group_passes = basis.shape[0] // K_PASS
+        assert group_passes % PAIR == 0
         passes.extend((group, i, group_passes) for i in range(group_passes))
     n_pairs = len(passes) // PAIR
-    n_chunks = n_pairs // CHUNK
-    assert len(passes) * K_PASS == target_grad.shape[1] and n_chunks * CHUNK * PAIR == len(passes)
+    assert len(passes) * K_PASS == target_grad.shape[1]
+
+    chunks = [(0, 1), (2, 3)] + [tuple(range(g, g + 4)) for g in range(4, n_pairs - 4, 4)]
+    chunks += [(n_pairs - 4, n_pairs - 3), (n_pairs - 2, n_pairs - 1)]
+    copy_step = [GRAD_DELAY + g * (n_pairs - 2 - GRAD_DELAY) // (n_pairs - 1) for g in range(n_pairs)]
 
     with ExitStack() as ctx:
         keep = ctx.enter_context(tc.tile_pool(name="keep", bufs=1))
         grad_pool = ctx.enter_context(tc.tile_pool(name="grad", bufs=3))
-        raw_pool = ctx.enter_context(tc.tile_pool(name="raw", bufs=6))
-        work = ctx.enter_context(tc.tile_pool(name="work", bufs=4))
+        raw_pool = ctx.enter_context(tc.tile_pool(name="raw", bufs=AHEAD + 2))
+        grouped_pool = ctx.enter_context(tc.tile_pool(name="grouped", bufs=3))
+        codes_pool = ctx.enter_context(tc.tile_pool(name="codes", bufs=6))
         acc_pool = ctx.enter_context(tc.psum_pool(name="acc", bufs=1))
         bank_pool = ctx.enter_context(tc.psum_pool(name="bank", bufs=5))
         ctx.enter_context(tc.manual_schedule())
@@ -58,70 +66,99 @@ def tile_gep_pa_kernel(tc, target_grad, bases0, bases1, bases2, out_0, out_1):
         grad_codes = keep.tile([P, len(passes) * P], U32, name="grad_codes", align_bytes=64)
         grad_scales = keep.tile([P, len(passes) * P], U8, name="grad_scales", align_bytes=64)
         sumsq = keep.tile([P, n_groups], F32, name="sumsq")
+        squares = keep.tile([P, width], F32, name="squares")
         embedding = [keep.tile([P, width], F32, name="embedding%d" % g) for g in range(n_groups)]
         acc = [acc_pool.tile([P, width], F32, name="acc%d" % g) for g in range(n_groups)]
 
-        flipped = {}
+        chunk_of = {}
+        for chunk in chunks:
+            chunk_of.update({pair: chunk for pair in chunk})
+        grad_raw = {}
         grad_grouped = {}
+        flipped = {}
 
-        def transpose_grad(chunk):
-            columns = CHUNK * PAIR * K_PASS
-            grad_raw = grad_pool.tile([P, columns], BF16, name="grad_raw")
-            nc.sync.dma_start(out=grad_raw[:], in_=target_grad[:, chunk * columns : (chunk + 1) * columns])
-            words = grad_raw[:].bitcast(F32).rearrange("b (c p u) -> b c u p", p=P, u=2)
-            flipped[chunk] = []
-            for pair in range(CHUNK):
-                bank = bank_pool.tile([P, PAIR, 2, P], F32, name="bank")
-                for c in range(PAIR):
-                    for u in range(2):
-                        nc.tensor.transpose(bank[:, c, u, :], words[:, pair * PAIR + c, u, :], identity[:])
-                flipped[chunk].append(bank)
+        def load_grad(even):
+            start = even * PAIR * K_PASS
+            columns = 2 * PAIR * K_PASS
+            grad_raw[even] = grad_pool.tile([P, columns], BF16, name="grad_raw")
+            nc.sync.dma_start(out=grad_raw[even][:], in_=target_grad[:, start : start + columns])
 
-        def copy_grad(chunk):
-            grad_grouped[chunk] = grad_pool.tile(
-                [P, CHUNK * PAIR * P * PACK], BF16, name="grad_grouped", align_bytes=64
-            )
-            grouped_words = grad_grouped[chunk][:].bitcast(F32).rearrange("p (c b u) -> p c b u", b=P, u=2)
-            for pair, bank in enumerate(flipped[chunk]):
-                nc.scalar.copy(
-                    out=grouped_words[:, pair * PAIR : (pair + 1) * PAIR],
-                    in_=bank[:].rearrange("p c u b -> p c b u"),
+        def transpose_grad(pair):
+            even = pair - pair % 2
+            words = grad_raw[even][:].bitcast(F32).rearrange("b (c p u) -> b c u p", p=P, u=2)
+            flipped[pair] = bank_pool.tile([P, PAIR, 2, P], F32, name="bank")
+            for c in range(PAIR):
+                for u in range(2):
+                    nc.tensor.transpose(
+                        flipped[pair][:, c, u, :], words[:, (pair - even) * PAIR + c, u, :], identity[:]
+                    )
+
+        def copy_grad(pair):
+            chunk = chunk_of[pair]
+            if chunk not in grad_grouped:
+                grad_grouped[chunk] = grad_pool.tile(
+                    [P, len(chunk) * PAIR * P * PACK], BF16, name="grad_grouped", align_bytes=64
                 )
+            words = grad_grouped[chunk][:].bitcast(F32).rearrange("p (c b u) -> p c b u", b=P, u=2)
+            begin = (pair - chunk[0]) * PAIR
+            nc.scalar.copy(
+                out=words[:, begin : begin + PAIR], in_=flipped[pair][:].rearrange("p c u b -> p c b u")
+            )
 
         def quantise_grad(chunk):
-            cols = slice(chunk * CHUNK * PAIR * P, (chunk + 1) * CHUNK * PAIR * P)
+            cols = slice(chunk[0] * PAIR * P, (chunk[-1] + 1) * PAIR * P)
             nc.vector.quantize_mx(
                 out=grad_codes[:, cols].bitcast(FP8X4), scales=grad_scales[:, cols], in_=grad_grouped[chunk][:]
             )
 
-        def load_basis(c, half):
-            group, i, group_passes = passes[c]
-            raw = raw_pool.tile([P, PACK, width], BF16, name="raw%d" % half)
-            rows = bases[group][i * K_PASS : (i + 1) * K_PASS, :]
-            nc.sync.dma_start(out=raw[:], in_=rows.rearrange("(p j) n -> p j n", j=PACK))
-            return raw
+        raw = {}
+        grouped = {}
+        codes = {}
+        scales = {}
 
-        def regroup(copy, raw, half):
-            grouped = work.tile([P, width, PACK], BF16, name="grouped%d" % half, align_bytes=64)
-            copy(
-                out=grouped[:].rearrange("p (c i) j -> p c j i", i=8),
-                in_=raw[:].rearrange("p j (c i) -> p c j i", i=8),
+        def load(pair, begin=0, end=PAIR):
+            group, i, group_passes = passes[pair * PAIR]
+            rows = bases[group][(i + begin) * K_PASS : (i + end) * K_PASS, :]
+            if begin == 0:
+                raw[pair] = raw_pool.tile([P, PAIR, PACK, width], BF16, name="raw")
+            nc.sync.dma_start(
+                out=raw[pair][:, begin:end], in_=rows.rearrange("(q p j) n -> p q j n", p=P, j=PACK)
             )
-            return grouped
 
-        def multiply(c, grouped):
-            group, i, group_passes = passes[c]
-            codes = work.tile([P, width], U32, name="codes", align_bytes=64)
-            scales = work.tile([P, width], U8, name="scales", align_bytes=64)
+        def regroup(pair, begin=0, end=PAIR):
+            if begin == 0:
+                grouped[pair] = grouped_pool.tile([P, PAIR, width, PACK], BF16, name="grouped", align_bytes=64)
+            for copy, cols in (
+                (nc.scalar.copy, slice(0, SCALAR_COLS)),
+                (nc.vector.tensor_copy, slice(SCALAR_COLS, width)),
+            ):
+                copy(
+                    out=grouped[pair][:, begin:end, cols].rearrange("p q (c i) j -> p q c j i", i=LINE),
+                    in_=raw[pair][:, begin:end, :, cols].rearrange("p q j (c i) -> p q c j i", i=LINE),
+                )
+
+        def quantise(pair, begin=0, end=PAIR):
+            if begin == 0:
+                codes[pair] = codes_pool.tile([P, PAIR * width], U32, name="codes", align_bytes=64)
+                scales[pair] = codes_pool.tile([P, PAIR * width], U8, name="scales", align_bytes=64)
+            cols = slice(begin * width, end * width)
             nc.vector.quantize_mx(
-                out=codes[:].bitcast(FP8X4), scales=scales[:], in_=grouped[:].rearrange("p n j -> p (n j)")
+                out=codes[pair][:, cols].bitcast(FP8X4),
+                scales=scales[pair][:, cols],
+                in_=grouped[pair][:, begin:end].rearrange("p q n j -> p (q n j)"),
             )
+
+        def multiply(pair, c):
+            index = pair * PAIR + c
+            group, i, group_passes = passes[index]
+            cols = slice(c * width, (c + 1) * width)
+            grad_cols = slice(index * P, (index + 1) * P)
             nc.tensor.matmul_mx(
                 out=acc[group][:],
-                lhsT=grad_codes[:, c * P : (c + 1) * P].bitcast(FP8X4),
-                lhsT_scale=grad_scales[:, c * P : (c + 1) * P],
-                rhs=codes[:].bitcast(FP8X4),
-                rhs_scale=scales[:],
+                lhsT=grad_codes[:, grad_cols].bitcast(FP8X4),
+                lhsT_scale=grad_scales[:, grad_cols],
+                rhs=codes[pair][:, cols].bitcast(FP8X4),
+                rhs_scale=scales[pair][:, cols],
                 start=(i == 0),
                 stop=(i == group_passes - 1),
             )
@@ -131,10 +168,9 @@ def tile_gep_pa_kernel(tc, target_grad, bases0, bases1, bases2, out_0, out_1):
             for unused in range(count):
                 nc.tensor.matmul(out=idle_acc[:], lhsT=zeros[:, :P], rhs=zeros[:], start=True, stop=True)
 
-        def sum_squares(group):
-            squares = work.tile([P, width], F32, name="squares")
+        def sum_squares(group, source):
             nc.scalar.activation(
-                out=squares[:], in_=acc[group][:], func=ACT.Square, accum_out=sumsq[:, group : group + 1]
+                out=squares[:], in_=source[:], func=ACT.Square, accum_out=sumsq[:, group : group + 1]
             )
 
         def copy_embedding(group):
@@ -143,35 +179,70 @@ def tile_gep_pa_kernel(tc, target_grad, bases0, bases1, bases2, out_0, out_1):
         def store_embedding(group):
             nc.sync.dma_start(out=out_0[:, group * width : (group + 1) * width], in_=embedding[group][:])
 
+        def load_step(step):
+            if step in (0, 1, n_pairs - 1):
+                for c in range(PAIR):
+                    load(step, c, c + 1)
+            else:
+                load(step)
+            for even in range(0, n_pairs, 2):
+                if step == copy_step[even] - 1:
+                    load_grad(even)
+
         last = n_groups - 1
-        for q in range(-4, n_pairs):
-            if q >= 0:
-                raw_first = load_basis(q * PAIR, 0)
-                raw_second = load_basis(q * PAIR + 1, 1)
-                grouped_first = regroup(nc.scalar.copy, raw_first, 0)
-                grouped_second = regroup(nc.vector.tensor_copy, raw_second, 1)
-                multiply(q * PAIR, grouped_first)
-                multiply(q * PAIR + 1, grouped_second)
-            if q % CHUNK == 1 and 0 <= (q + 1) // CHUNK < n_chunks:
-                quantise_grad((q + 1) // CHUNK)
-            if q % CHUNK == 0 and 0 <= (q + 2) // CHUNK < n_chunks:
-                copy_grad((q + 2) // CHUNK)
-            if q % CHUNK == 0 and 0 <= (q + 4) // CHUNK < n_chunks:
-                transpose_grad((q + 4) // CHUNK)
-            if q >= 1:
-                group, i, group_passes = passes[q * PAIR - 1]
-                if i == group_passes - 1:
-                    sum_squares(group)
-                    copy_embedding(group)
-            if q == n_pairs - 2:
-                keep_clock(2)
+        for step in range(AHEAD):
+            load_step(step)
+        multiplied = 0
+        quantised = set()
+        closed_at = {}
+        for step in range(n_pairs):
+            if step + AHEAD < n_pairs:
+                load_step(step + AHEAD)
+
+            if step < n_pairs - 1:
+                regroup(step)
+            else:
+                regroup(step, 0, 1)
+            for pair in range(n_pairs):
+                if copy_step[pair] == step:
+                    copy_grad(pair)
+            for chunk in chunks:
+                if copy_step[chunk[-1]] == step - 1:
+                    quantise_grad(chunk)
+                    quantised.add(chunk)
+            if step >= 1:
+                quantise(step - 1)
+            if step == n_pairs - 1:
+                regroup(step, 1, 2)
+                quantise(step, 0, 1)
+                quantise(step, 1, 2)
+
+            for pair in range(n_pairs):
+                if copy_step[pair] == step + 1:
+                    transpose_grad(pair)
+            while multiplied < step and chunk_of[multiplied] in quantised:
+                for c in range(PAIR):
+                    multiply(multiplied, c)
+                    group, i, group_passes = passes[multiplied * PAIR + c]
+                    if i == group_passes - 1:
+                        closed_at[step] = group
+                multiplied += 1
+
+            if step - 1 in closed_at:
+                copy_embedding(closed_at[step - 1])
+            if step - 2 in closed_at:
+                sum_squares(closed_at[step - 2], embedding[closed_at[step - 2]])
 
         for group in range(last):
             store_embedding(group)
 
+        for c in range(PAIR):
+            keep_clock(1)
+            multiply(n_pairs - 1, c)
+
         early = keep.tile([P, 1], F32, name="early")
         nc.vector.tensor_reduce(out=early[:], in_=sumsq[:, :last], op=ALU.add, axis=mybir.AxisListType.X)
-        sum_squares(last)
+        sum_squares(last, acc[last])
         keep_clock(3)
         inverse = keep.tile([P, 1], F32, name="inverse")
         nc.scalar.activation(

@@ -14,11 +14,12 @@ ALU = mybir.AluOpType
 P = 128
 PACK = 4
 K_PASS = P * PACK
-PAIR = 2
+QUAD = 4
+SIDES = 2
 LINE = 8
-SCALAR_COLS = 240
-AHEAD = 6
-GRAD_DELAY = 2
+SCALAR_COLS = 272
+MID_COLS = 448
+FIRST_COLS = 192
 CLIP = 1.0
 
 FLOPS = 2 * 128 * 20480 * 512 + 2 * 128 * 1536
@@ -33,21 +34,19 @@ def tile_gep_pa_kernel(tc, target_grad, bases0, bases1, bases2, out_0, out_1):
     passes = []
     for group, basis in enumerate(bases):
         group_passes = basis.shape[0] // K_PASS
-        assert group_passes % PAIR == 0
         passes.extend((group, i, group_passes) for i in range(group_passes))
-    n_pairs = len(passes) // PAIR
-    assert len(passes) * K_PASS == target_grad.shape[1]
+    n_quads = len(passes) // QUAD
+    final = n_quads - 1
+    assert len(passes) * K_PASS == target_grad.shape[1] and n_quads * QUAD == len(passes)
 
-    chunks = [(0, 1), (2, 3)] + [tuple(range(g, g + 4)) for g in range(4, n_pairs - 4, 4)]
-    chunks += [(n_pairs - 4, n_pairs - 3), (n_pairs - 2, n_pairs - 1)]
-    copy_step = [GRAD_DELAY + g * (n_pairs - 2 - GRAD_DELAY) // (n_pairs - 1) for g in range(n_pairs)]
+    grad_step = [1 + (7 * quad + 4) // 9 for quad in range(n_quads)]
 
     with ExitStack() as ctx:
         keep = ctx.enter_context(tc.tile_pool(name="keep", bufs=1))
-        grad_pool = ctx.enter_context(tc.tile_pool(name="grad", bufs=3))
-        raw_pool = ctx.enter_context(tc.tile_pool(name="raw", bufs=AHEAD + 2))
-        grouped_pool = ctx.enter_context(tc.tile_pool(name="grouped", bufs=3))
-        codes_pool = ctx.enter_context(tc.tile_pool(name="codes", bufs=6))
+        grad_pool = ctx.enter_context(tc.tile_pool(name="grad", bufs=2))
+        raw_pool = ctx.enter_context(tc.tile_pool(name="raw", bufs=6))
+        grouped_pool = ctx.enter_context(tc.tile_pool(name="grouped", bufs=2))
+        codes_pool = ctx.enter_context(tc.tile_pool(name="codes", bufs=4))
         acc_pool = ctx.enter_context(tc.psum_pool(name="acc", bufs=1))
         bank_pool = ctx.enter_context(tc.psum_pool(name="bank", bufs=5))
         ctx.enter_context(tc.manual_schedule())
@@ -70,45 +69,46 @@ def tile_gep_pa_kernel(tc, target_grad, bases0, bases1, bases2, out_0, out_1):
         embedding = [keep.tile([P, width], F32, name="embedding%d" % g) for g in range(n_groups)]
         acc = [acc_pool.tile([P, width], F32, name="acc%d" % g) for g in range(n_groups)]
 
-        chunk_of = {}
-        for chunk in chunks:
-            chunk_of.update({pair: chunk for pair in chunk})
+        chunks = {}
+        for quad in range(n_quads):
+            chunks.setdefault(grad_step[quad], []).append(quad)
         grad_raw = {}
         grad_grouped = {}
         flipped = {}
 
-        def load_grad(even):
-            start = even * PAIR * K_PASS
-            columns = 2 * PAIR * K_PASS
-            grad_raw[even] = grad_pool.tile([P, columns], BF16, name="grad_raw")
-            nc.sync.dma_start(out=grad_raw[even][:], in_=target_grad[:, start : start + columns])
+        def load_grad(step):
+            start = chunks[step][0] * QUAD * K_PASS
+            columns = len(chunks[step]) * QUAD * K_PASS
+            grad_raw[step] = grad_pool.tile([P, columns], BF16, name="grad_raw")
+            nc.sync.dma_start(out=grad_raw[step][:], in_=target_grad[:, start : start + columns])
 
-        def transpose_grad(pair):
-            even = pair - pair % 2
-            words = grad_raw[even][:].bitcast(F32).rearrange("b (c p u) -> b c u p", p=P, u=2)
-            flipped[pair] = bank_pool.tile([P, PAIR, 2, P], F32, name="bank")
-            for c in range(PAIR):
-                for u in range(2):
-                    nc.tensor.transpose(
-                        flipped[pair][:, c, u, :], words[:, (pair - even) * PAIR + c, u, :], identity[:]
-                    )
+        def transpose_grad(step):
+            words = grad_raw[step][:].bitcast(F32).rearrange("b (c p u) -> b c u p", p=P, u=2)
+            for index, quad in enumerate(chunks[step]):
+                flipped[quad] = []
+                for first in (0, 2):
+                    bank = bank_pool.tile([P, 2, 2, P], F32, name="bank")
+                    for c in range(2):
+                        for u in range(2):
+                            nc.tensor.transpose(
+                                bank[:, c, u, :], words[:, index * QUAD + first + c, u, :], identity[:]
+                            )
+                    flipped[quad].append(bank)
 
-        def copy_grad(pair):
-            chunk = chunk_of[pair]
-            if chunk not in grad_grouped:
-                grad_grouped[chunk] = grad_pool.tile(
-                    [P, len(chunk) * PAIR * P * PACK], BF16, name="grad_grouped", align_bytes=64
-                )
-            words = grad_grouped[chunk][:].bitcast(F32).rearrange("p (c b u) -> p c b u", b=P, u=2)
-            begin = (pair - chunk[0]) * PAIR
-            nc.scalar.copy(
-                out=words[:, begin : begin + PAIR], in_=flipped[pair][:].rearrange("p c u b -> p c b u")
+        def copy_grad(step):
+            grad_grouped[step] = grad_pool.tile(
+                [P, len(chunks[step]) * QUAD * P * PACK], BF16, name="grad_grouped", align_bytes=64
             )
+            words = grad_grouped[step][:].bitcast(F32).rearrange("p (c b u) -> p c b u", b=P, u=2)
+            for index, quad in enumerate(chunks[step]):
+                for half, bank in enumerate(flipped[quad]):
+                    begin = index * QUAD + 2 * half
+                    nc.scalar.copy(out=words[:, begin : begin + 2], in_=bank[:].rearrange("p c u b -> p c b u"))
 
-        def quantise_grad(chunk):
-            cols = slice(chunk[0] * PAIR * P, (chunk[-1] + 1) * PAIR * P)
+        def quantise_grad(step):
+            cols = slice(chunks[step][0] * QUAD * P, (chunks[step][-1] + 1) * QUAD * P)
             nc.vector.quantize_mx(
-                out=grad_codes[:, cols].bitcast(FP8X4), scales=grad_scales[:, cols], in_=grad_grouped[chunk][:]
+                out=grad_codes[:, cols].bitcast(FP8X4), scales=grad_scales[:, cols], in_=grad_grouped[step][:]
             )
 
         raw = {}
@@ -116,49 +116,48 @@ def tile_gep_pa_kernel(tc, target_grad, bases0, bases1, bases2, out_0, out_1):
         codes = {}
         scales = {}
 
-        def load(pair, begin=0, end=PAIR):
-            group, i, group_passes = passes[pair * PAIR]
-            rows = bases[group][(i + begin) * K_PASS : (i + end) * K_PASS, :]
-            if begin == 0:
-                raw[pair] = raw_pool.tile([P, PAIR, PACK, width], BF16, name="raw")
-            nc.sync.dma_start(
-                out=raw[pair][:, begin:end], in_=rows.rearrange("(q p j) n -> p q j n", p=P, j=PACK)
+        def load(index):
+            group, i, group_passes = passes[index]
+            raw[index] = raw_pool.tile([P, PACK, width], BF16, name="raw%d" % (index % SIDES))
+            rows = bases[group][i * K_PASS : (i + 1) * K_PASS, :]
+            nc.sync.dma_start(out=raw[index][:], in_=rows.rearrange("(p j) n -> p j n", j=PACK))
+
+        def regroup(copy, index, begin, end):
+            quad, c = divmod(index, QUAD)
+            key = (quad, c % SIDES)
+            if key not in grouped:
+                grouped[key] = grouped_pool.tile(
+                    [P, 2, width, PACK], BF16, name="grouped%d" % key[1], align_bytes=64
+                )
+            copy(
+                out=grouped[key][:, c // SIDES, begin:end].rearrange("p (c i) j -> p c j i", i=LINE),
+                in_=raw[index][:, :, begin:end].rearrange("p j (c i) -> p c j i", i=LINE),
             )
 
-        def regroup(pair, begin=0, end=PAIR):
-            if begin == 0:
-                grouped[pair] = grouped_pool.tile([P, PAIR, width, PACK], BF16, name="grouped", align_bytes=64)
-            for copy, cols in (
-                (nc.scalar.copy, slice(0, SCALAR_COLS)),
-                (nc.vector.tensor_copy, slice(SCALAR_COLS, width)),
-            ):
-                copy(
-                    out=grouped[pair][:, begin:end, cols].rearrange("p q (c i) j -> p q c j i", i=LINE),
-                    in_=raw[pair][:, begin:end, :, cols].rearrange("p q j (c i) -> p q c j i", i=LINE),
-                )
-
-        def quantise(pair, begin=0, end=PAIR):
-            if begin == 0:
-                codes[pair] = codes_pool.tile([P, PAIR * width], U32, name="codes", align_bytes=64)
-                scales[pair] = codes_pool.tile([P, PAIR * width], U8, name="scales", align_bytes=64)
+        def quantise(quad, side, begin=0, end=2):
+            key = (quad, side)
+            if key not in codes:
+                codes[key] = codes_pool.tile([P, 2 * width], U32, name="codes%d" % side, align_bytes=64)
+                scales[key] = codes_pool.tile([P, 2 * width], U8, name="scales%d" % side, align_bytes=64)
             cols = slice(begin * width, end * width)
             nc.vector.quantize_mx(
-                out=codes[pair][:, cols].bitcast(FP8X4),
-                scales=scales[pair][:, cols],
-                in_=grouped[pair][:, begin:end].rearrange("p q n j -> p (q n j)"),
+                out=codes[key][:, cols].bitcast(FP8X4),
+                scales=scales[key][:, cols],
+                in_=grouped[key][:, begin:end].rearrange("p q n j -> p (q n j)"),
             )
 
-        def multiply(pair, c):
-            index = pair * PAIR + c
+        def multiply(index):
             group, i, group_passes = passes[index]
-            cols = slice(c * width, (c + 1) * width)
+            quad, c = divmod(index, QUAD)
+            key = (quad, c % SIDES)
+            cols = slice((c // SIDES) * width, (c // SIDES + 1) * width)
             grad_cols = slice(index * P, (index + 1) * P)
             nc.tensor.matmul_mx(
                 out=acc[group][:],
                 lhsT=grad_codes[:, grad_cols].bitcast(FP8X4),
                 lhsT_scale=grad_scales[:, grad_cols],
-                rhs=codes[pair][:, cols].bitcast(FP8X4),
-                rhs_scale=scales[pair][:, cols],
+                rhs=codes[key][:, cols].bitcast(FP8X4),
+                rhs_scale=scales[key][:, cols],
                 start=(i == 0),
                 stop=(i == group_passes - 1),
             )
@@ -168,9 +167,9 @@ def tile_gep_pa_kernel(tc, target_grad, bases0, bases1, bases2, out_0, out_1):
             for unused in range(count):
                 nc.tensor.matmul(out=idle_acc[:], lhsT=zeros[:, :P], rhs=zeros[:], start=True, stop=True)
 
-        def sum_squares(group, source):
+        def sum_squares(group):
             nc.scalar.activation(
-                out=squares[:], in_=source[:], func=ACT.Square, accum_out=sumsq[:, group : group + 1]
+                out=squares[:], in_=acc[group][:], func=ACT.Square, accum_out=sumsq[:, group : group + 1]
             )
 
         def copy_embedding(group):
@@ -179,70 +178,80 @@ def tile_gep_pa_kernel(tc, target_grad, bases0, bases1, bases2, out_0, out_1):
         def store_embedding(group):
             nc.sync.dma_start(out=out_0[:, group * width : (group + 1) * width], in_=embedding[group][:])
 
-        def load_step(step):
-            if step in (0, 1, n_pairs - 1):
-                for c in range(PAIR):
-                    load(step, c, c + 1)
-            else:
-                load(step)
-            for even in range(0, n_pairs, 2):
-                if step == copy_step[even] - 1:
-                    load_grad(even)
-
         last = n_groups - 1
-        for step in range(AHEAD):
-            load_step(step)
-        multiplied = 0
-        quantised = set()
+        scalar_copy, vector_copy = nc.scalar.copy, nc.vector.tensor_copy
+        ready = []
         closed_at = {}
-        for step in range(n_pairs):
-            if step + AHEAD < n_pairs:
-                load_step(step + AHEAD)
+        for step in range(n_quads):
+            indices = [step * QUAD + c for c in range(QUAD)]
+            for index in indices:
+                load(index)
+            if step + 1 in chunks:
+                load_grad(step + 1)
 
-            if step < n_pairs - 1:
-                regroup(step)
+            if step < final:
+                if step == 0:
+                    regroup(scalar_copy, 0, 0, FIRST_COLS)
+                for index in indices[1::2]:
+                    regroup(scalar_copy, index, 0, MID_COLS if step and index == indices[3] else width)
             else:
-                regroup(step, 0, 1)
-            for pair in range(n_pairs):
-                if copy_step[pair] == step:
-                    copy_grad(pair)
-            for chunk in chunks:
-                if copy_step[chunk[-1]] == step - 1:
-                    quantise_grad(chunk)
-                    quantised.add(chunk)
-            if step >= 1:
-                quantise(step - 1)
-            if step == n_pairs - 1:
-                regroup(step, 1, 2)
-                quantise(step, 0, 1)
-                quantise(step, 1, 2)
+                for index in indices:
+                    regroup(scalar_copy, index, 0, SCALAR_COLS)
 
-            for pair in range(n_pairs):
-                if copy_step[pair] == step + 1:
-                    transpose_grad(pair)
-            while multiplied < step and chunk_of[multiplied] in quantised:
-                for c in range(PAIR):
-                    multiply(multiplied, c)
-                    group, i, group_passes = passes[multiplied * PAIR + c]
-                    if i == group_passes - 1:
-                        closed_at[step] = group
-                multiplied += 1
+            if step + 1 in chunks:
+                transpose_grad(step + 1)
+                copy_grad(step + 1)
+
+            if step < final:
+                regroup(vector_copy, indices[0], FIRST_COLS if step == 0 else 0, width)
+                if step == 0:
+                    quantise(step, 0, 0, 1)
+                else:
+                    quantise(step - 1, 1)
+                regroup(vector_copy, indices[2], 0, width)
+                if step:
+                    regroup(vector_copy, indices[3], MID_COLS, width)
+                if step in chunks:
+                    quantise_grad(step)
+                if step == 0:
+                    quantise(step, 0, 1, 2)
+                else:
+                    quantise(step, 0)
+                if step > 0:
+                    ready += [(step - 1) * QUAD + c for c in (1, 3)]
+                ready += indices[0::2]
+                waiting = []
+                for index in ready:
+                    if grad_step[index // QUAD] <= step:
+                        multiply(index)
+                        if passes[index][1] == passes[index][2] - 1:
+                            closed_at[step] = passes[index][0]
+                    else:
+                        waiting.append(index)
+                ready = waiting
+            else:
+                for c, index in enumerate(indices):
+                    regroup(vector_copy, index, SCALAR_COLS, width)
+                    if c == 0:
+                        quantise(step - 1, 1)
+                    else:
+                        quantise(step, (c - 1) % SIDES, (c - 1) // SIDES, (c - 1) // SIDES + 1)
+                quantise(step, 1, 1, 2)
+                for index in ready + [(step - 1) * QUAD + c for c in (1, 3)]:
+                    multiply(index)
 
             if step - 1 in closed_at:
-                copy_embedding(closed_at[step - 1])
-            if step - 2 in closed_at:
-                sum_squares(closed_at[step - 2], embedding[closed_at[step - 2]])
+                sum_squares(closed_at[step - 1])
 
-        for group in range(last):
-            store_embedding(group)
-
-        for c in range(PAIR):
-            keep_clock(1)
-            multiply(n_pairs - 1, c)
+        for c, index in enumerate(indices):
+            if c:
+                keep_clock(1)
+            multiply(index)
 
         early = keep.tile([P, 1], F32, name="early")
         nc.vector.tensor_reduce(out=early[:], in_=sumsq[:, :last], op=ALU.add, axis=mybir.AxisListType.X)
-        sum_squares(last, acc[last])
+        sum_squares(last)
+        copy_embedding(0)
         keep_clock(3)
         inverse = keep.tile([P, 1], F32, name="inverse")
         nc.scalar.activation(
@@ -252,8 +261,10 @@ def tile_gep_pa_kernel(tc, target_grad, bases0, bases1, bases2, out_0, out_1):
         nc.vector.tensor_scalar(
             out=factor[:], in0=inverse[:], scalar1=CLIP / P, scalar2=1.0 / P, op0=ALU.mult, op1=ALU.min
         )
-        copy_embedding(last)
-        store_embedding(last)
+        for group in range(1, n_groups):
+            copy_embedding(group)
+        for group in range(n_groups):
+            store_embedding(group)
 
         mean = keep.tile([P, n_groups * width], F32, name="mean")
         half = width // 2

@@ -17,9 +17,10 @@ K_PASS = P * PACK
 QUAD = 4
 SIDES = 2
 LINE = 8
-SCALAR_COLS = 272
-MID_COLS = 448
+SCALAR_COLS = 256
+MID_COLS = 464
 FIRST_COLS = 192
+LATE = 2
 CLIP = 1.0
 
 FLOPS = 2 * 128 * 20480 * 512 + 2 * 128 * 1536
@@ -39,7 +40,7 @@ def tile_gep_pa_kernel(tc, target_grad, bases0, bases1, bases2, out_0, out_1):
     final = n_quads - 1
     assert len(passes) * K_PASS == target_grad.shape[1] and n_quads * QUAD == len(passes)
 
-    grad_step = [1 + (7 * quad + 4) // 9 for quad in range(n_quads)]
+    grad_step = [quad + (quad < n_quads - LATE) for quad in range(n_quads)]
 
     with ExitStack() as ctx:
         keep = ctx.enter_context(tc.tile_pool(name="keep", bufs=1))
@@ -48,7 +49,7 @@ def tile_gep_pa_kernel(tc, target_grad, bases0, bases1, bases2, out_0, out_1):
         grouped_pool = ctx.enter_context(tc.tile_pool(name="grouped", bufs=2))
         codes_pool = ctx.enter_context(tc.tile_pool(name="codes", bufs=4))
         acc_pool = ctx.enter_context(tc.psum_pool(name="acc", bufs=1))
-        bank_pool = ctx.enter_context(tc.psum_pool(name="bank", bufs=5))
+        bank_pool = ctx.enter_context(tc.psum_pool(name="bank", bufs=4))
         ctx.enter_context(tc.manual_schedule())
 
         identity = keep.tile([P, P], F32, name="identity")
@@ -64,10 +65,12 @@ def tile_gep_pa_kernel(tc, target_grad, bases0, bases1, bases2, out_0, out_1):
 
         grad_codes = keep.tile([P, len(passes) * P], U32, name="grad_codes", align_bytes=64)
         grad_scales = keep.tile([P, len(passes) * P], U8, name="grad_scales", align_bytes=64)
-        sumsq = keep.tile([P, n_groups], F32, name="sumsq")
+        halves = [slice(0, width // 2), slice(width // 2, width)]
+        parts = [(group, slice(0, width)) for group in range(n_groups - 1)] + [(n_groups - 1, cols) for cols in halves]
+        sumsq = keep.tile([P, len(parts)], F32, name="sumsq")
         squares = keep.tile([P, width], F32, name="squares")
         embedding = [keep.tile([P, width], F32, name="embedding%d" % g) for g in range(n_groups)]
-        acc = [acc_pool.tile([P, width], F32, name="acc%d" % g) for g in range(n_groups)]
+        acc = [acc_pool.tile([P, width], F32, name="acc%d" % part) for part in range(len(parts))]
 
         chunks = {}
         for quad in range(n_quads):
@@ -77,10 +80,13 @@ def tile_gep_pa_kernel(tc, target_grad, bases0, bases1, bases2, out_0, out_1):
         flipped = {}
 
         def load_grad(step):
-            start = chunks[step][0] * QUAD * K_PASS
-            columns = len(chunks[step]) * QUAD * K_PASS
-            grad_raw[step] = grad_pool.tile([P, columns], BF16, name="grad_raw")
-            nc.sync.dma_start(out=grad_raw[step][:], in_=target_grad[:, start : start + columns])
+            columns = QUAD * K_PASS
+            grad_raw[step] = grad_pool.tile([P, len(chunks[step]) * columns], BF16, name="grad_raw")
+            for index, quad in enumerate(chunks[step]):
+                nc.sync.dma_start(
+                    out=grad_raw[step][:, index * columns : (index + 1) * columns],
+                    in_=target_grad[:, quad * columns : (quad + 1) * columns],
+                )
 
         def transpose_grad(step):
             words = grad_raw[step][:].bitcast(F32).rearrange("b (c p u) -> b c u p", p=P, u=2)
@@ -134,6 +140,17 @@ def tile_gep_pa_kernel(tc, target_grad, bases0, bases1, bases2, out_0, out_1):
                 in_=raw[index][:, :, begin:end].rearrange("p j (c i) -> p c j i", i=LINE),
             )
 
+        def quantise_half(index, cols):
+            quad, c = divmod(index, QUAD)
+            key = (quad, c % SIDES)
+            base = (c // SIDES) * width
+            words = slice(base + cols.start, base + cols.stop)
+            nc.vector.quantize_mx(
+                out=codes[key][:, words].bitcast(FP8X4),
+                scales=scales[key][:, words],
+                in_=grouped[key][:, c // SIDES, cols].rearrange("p n j -> p (n j)"),
+            )
+
         def quantise(quad, side, begin=0, end=2):
             key = (quad, side)
             if key not in codes:
@@ -146,34 +163,42 @@ def tile_gep_pa_kernel(tc, target_grad, bases0, bases1, bases2, out_0, out_1):
                 in_=grouped[key][:, begin:end].rearrange("p q n j -> p (q n j)"),
             )
 
-        def multiply(index):
+        def multiply(index, chosen=None):
             group, i, group_passes = passes[index]
             quad, c = divmod(index, QUAD)
             key = (quad, c % SIDES)
-            cols = slice((c // SIDES) * width, (c // SIDES + 1) * width)
+            base = (c // SIDES) * width
             grad_cols = slice(index * P, (index + 1) * P)
-            nc.tensor.matmul_mx(
-                out=acc[group][:],
-                lhsT=grad_codes[:, grad_cols].bitcast(FP8X4),
-                lhsT_scale=grad_scales[:, grad_cols],
-                rhs=codes[key][:, cols].bitcast(FP8X4),
-                rhs_scale=scales[key][:, cols],
-                start=(i == 0),
-                stop=(i == group_passes - 1),
-            )
+            for part, (owner, cols) in enumerate(parts):
+                if owner == group and chosen in (None, part):
+                    words = slice(base + cols.start, base + cols.stop)
+                    nc.tensor.matmul_mx(
+                        out=acc[part][:, : cols.stop - cols.start],
+                        lhsT=grad_codes[:, grad_cols].bitcast(FP8X4),
+                        lhsT_scale=grad_scales[:, grad_cols],
+                        rhs=codes[key][:, words].bitcast(FP8X4),
+                        rhs_scale=scales[key][:, words],
+                        start=(i == 0),
+                        stop=(i == group_passes - 1),
+                    )
 
         def keep_clock(count):
             idle_acc = bank_pool.tile([P, width], F32, name="idle_acc", tag="bank")
             for unused in range(count):
                 nc.tensor.matmul(out=idle_acc[:], lhsT=zeros[:, :P], rhs=zeros[:], start=True, stop=True)
 
-        def sum_squares(group):
+        def sum_squares(part):
+            cols = parts[part][1]
             nc.scalar.activation(
-                out=squares[:], in_=acc[group][:], func=ACT.Square, accum_out=sumsq[:, group : group + 1]
+                out=squares[:, cols],
+                in_=acc[part][:, : cols.stop - cols.start],
+                func=ACT.Square,
+                accum_out=sumsq[:, part : part + 1],
             )
 
-        def copy_embedding(group):
-            nc.vector.tensor_copy(out=embedding[group][:], in_=acc[group][:])
+        def copy_embedding(part):
+            group, cols = parts[part]
+            nc.vector.tensor_copy(out=embedding[group][:, cols], in_=acc[part][:, : cols.stop - cols.start])
 
         def store_embedding(group):
             nc.sync.dma_start(out=out_0[:, group * width : (group + 1) * width], in_=embedding[group][:])
@@ -184,21 +209,28 @@ def tile_gep_pa_kernel(tc, target_grad, bases0, bases1, bases2, out_0, out_1):
         closed_at = {}
         for step in range(n_quads):
             indices = [step * QUAD + c for c in range(QUAD)]
-            for index in indices:
+            for index in indices[:2]:
                 load(index)
-            if step + 1 in chunks:
+            if step == 1:
+                load_grad(1)
+            for index in indices[2:]:
+                load(index)
+            if step and step + 1 in chunks:
                 load_grad(step + 1)
 
             if step < final:
                 if step == 0:
                     regroup(scalar_copy, 0, 0, FIRST_COLS)
-                for index in indices[1::2]:
-                    regroup(scalar_copy, index, 0, MID_COLS if step and index == indices[3] else width)
+                regroup(scalar_copy, indices[1], 0, width)
+                if step == 1:
+                    transpose_grad(1)
+                    copy_grad(1)
+                regroup(scalar_copy, indices[3], 0, MID_COLS if step else width)
             else:
                 for index in indices:
                     regroup(scalar_copy, index, 0, SCALAR_COLS)
 
-            if step + 1 in chunks:
+            if step and step + 1 in chunks:
                 transpose_grad(step + 1)
                 copy_grad(step + 1)
 
@@ -236,48 +268,55 @@ def tile_gep_pa_kernel(tc, target_grad, bases0, bases1, bases2, out_0, out_1):
                         quantise(step - 1, 1)
                     else:
                         quantise(step, (c - 1) % SIDES, (c - 1) // SIDES, (c - 1) // SIDES + 1)
-                quantise(step, 1, 1, 2)
+                    if c == 1:
+                        quantise_grad(step)
                 for index in ready + [(step - 1) * QUAD + c for c in (1, 3)]:
                     multiply(index)
 
             if step - 1 in closed_at:
                 sum_squares(closed_at[step - 1])
 
-        for c, index in enumerate(indices):
+        for c, index in enumerate(indices[:-1]):
             if c:
                 keep_clock(1)
             multiply(index)
+        for part, (group, cols) in enumerate(parts):
+            if group == last:
+                quantise_half(indices[-1], cols)
+                multiply(indices[-1], part)
 
         early = keep.tile([P, 1], F32, name="early")
-        nc.vector.tensor_reduce(out=early[:], in_=sumsq[:, :last], op=ALU.add, axis=mybir.AxisListType.X)
-        sum_squares(last)
+        final_part = len(parts) - 1
+        sum_squares(final_part - 1)
+        nc.vector.tensor_reduce(out=early[:], in_=sumsq[:, :final_part], op=ALU.add, axis=mybir.AxisListType.X)
+        sum_squares(final_part)
         copy_embedding(0)
-        keep_clock(3)
+        keep_clock(2)
         inverse = keep.tile([P, 1], F32, name="inverse")
         nc.scalar.activation(
-            out=inverse[:], in_=sumsq[:, last : last + 1], func=ACT.Abs_reciprocal_sqrt, bias=early[:]
+            out=inverse[:], in_=sumsq[:, final_part:], func=ACT.Abs_reciprocal_sqrt, bias=early[:]
         )
         factor = keep.tile([P, 1], F32, name="factor")
         nc.vector.tensor_scalar(
             out=factor[:], in0=inverse[:], scalar1=CLIP / P, scalar2=1.0 / P, op0=ALU.mult, op1=ALU.min
         )
-        for group in range(1, n_groups):
-            copy_embedding(group)
+        for part in range(1, len(parts)):
+            copy_embedding(part)
         for group in range(n_groups):
             store_embedding(group)
 
         mean = keep.tile([P, n_groups * width], F32, name="mean")
-        half = width // 2
-        parts = [(group, 0, width) for group in range(last)] + [(last, 0, half), (last, half, width)]
-        for index, (group, begin, end) in enumerate(parts):
+        for part, (group, cols) in enumerate(parts):
+            count = cols.stop - cols.start
             mean_acc = bank_pool.tile([P, width], F32, name="mean_acc", tag="bank")
             nc.tensor.matmul(
-                out=mean_acc[:, : end - begin],
+                out=mean_acc[:, :count],
                 lhsT=factor[:, 0:1].to_broadcast([P, P]),
-                rhs=embedding[group][:, begin:end],
+                rhs=embedding[group][:, cols],
                 start=True,
                 stop=True,
             )
-            copy = nc.scalar.copy if index % 2 else nc.vector.tensor_copy
-            copy(out=mean[:, group * width + begin : group * width + end], in_=mean_acc[:, : end - begin])
+            copy = nc.scalar.copy if part % 2 else nc.vector.tensor_copy
+            start = group * width + cols.start
+            copy(out=mean[:, start : start + count], in_=mean_acc[:, :count])
         nc.sync.dma_start(out=out_1.rearrange("(o n) -> o n", o=1), in_=mean[0:1, :])

@@ -17,10 +17,10 @@ K_PASS = P * PACK
 QUAD = 4
 SIDES = 2
 LINE = 8
-SCALAR_COLS = 256
+SCALAR_COLS = (256, 272, 288, 304)
 MID_COLS = 464
 FIRST_COLS = 192
-LATE = 2
+LATE = 5
 CLIP = 1.0
 
 FLOPS = 2 * 128 * 20480 * 512 + 2 * 128 * 1536
@@ -67,7 +67,9 @@ def tile_gep_pa_kernel(tc, target_grad, bases0, bases1, bases2, out_0, out_1):
         grad_scales = keep.tile([P, len(passes) * P], U8, name="grad_scales", align_bytes=64)
         halves = [slice(0, width // 2), slice(width // 2, width)]
         parts = [(group, slice(0, width)) for group in range(n_groups - 1)] + [(n_groups - 1, cols) for cols in halves]
-        sumsq = keep.tile([P, len(parts)], F32, name="sumsq")
+        last_part = len(parts) - 1
+        sumsq = keep.tile([P, len(parts) + 1], F32, name="sumsq")
+        nc.vector.memset(sumsq[:, last_part : last_part + 1], -CLIP * CLIP)
         squares = keep.tile([P, width], F32, name="squares")
         embedding = [keep.tile([P, width], F32, name="embedding%d" % g) for g in range(n_groups)]
         acc = [acc_pool.tile([P, width], F32, name="acc%d" % part) for part in range(len(parts))]
@@ -193,7 +195,7 @@ def tile_gep_pa_kernel(tc, target_grad, bases0, bases1, bases2, out_0, out_1):
                 out=squares[:, cols],
                 in_=acc[part][:, : cols.stop - cols.start],
                 func=ACT.Square,
-                accum_out=sumsq[:, part : part + 1],
+                accum_out=sumsq[:, part + (part == last_part) : part + (part == last_part) + 1],
             )
 
         def copy_embedding(part):
@@ -227,8 +229,8 @@ def tile_gep_pa_kernel(tc, target_grad, bases0, bases1, bases2, out_0, out_1):
                     copy_grad(1)
                 regroup(scalar_copy, indices[3], 0, MID_COLS if step else width)
             else:
-                for index in indices:
-                    regroup(scalar_copy, index, 0, SCALAR_COLS)
+                for c, index in enumerate(indices):
+                    regroup(scalar_copy, index, 0, SCALAR_COLS[c])
 
             if step and step + 1 in chunks:
                 transpose_grad(step + 1)
@@ -263,7 +265,7 @@ def tile_gep_pa_kernel(tc, target_grad, bases0, bases1, bases2, out_0, out_1):
                 ready = waiting
             else:
                 for c, index in enumerate(indices):
-                    regroup(vector_copy, index, SCALAR_COLS, width)
+                    regroup(vector_copy, index, SCALAR_COLS[c], width)
                     if c == 0:
                         quantise(step - 1, 1)
                     else:
@@ -286,19 +288,18 @@ def tile_gep_pa_kernel(tc, target_grad, bases0, bases1, bases2, out_0, out_1):
                 multiply(indices[-1], part)
 
         early = keep.tile([P, 1], F32, name="early")
-        final_part = len(parts) - 1
-        sum_squares(final_part - 1)
-        nc.vector.tensor_reduce(out=early[:], in_=sumsq[:, :final_part], op=ALU.add, axis=mybir.AxisListType.X)
-        sum_squares(final_part)
+        sum_squares(last_part - 1)
+        nc.vector.tensor_reduce(
+            out=early[:], in_=sumsq[:, : last_part + 1], op=ALU.add, axis=mybir.AxisListType.X
+        )
+        sum_squares(last_part)
         copy_embedding(0)
         keep_clock(2)
-        inverse = keep.tile([P, 1], F32, name="inverse")
-        nc.scalar.activation(
-            out=inverse[:], in_=sumsq[:, final_part:], func=ACT.Abs_reciprocal_sqrt, bias=early[:]
-        )
+        excess = keep.tile([P, 1], F32, name="excess")
+        nc.scalar.activation(out=excess[:], in_=sumsq[:, last_part + 1 :], func=ACT.Relu, bias=early[:])
         factor = keep.tile([P, 1], F32, name="factor")
-        nc.vector.tensor_scalar(
-            out=factor[:], in0=inverse[:], scalar1=CLIP / P, scalar2=1.0 / P, op0=ALU.mult, op1=ALU.min
+        nc.scalar.activation(
+            out=factor[:], in_=excess[:], func=ACT.Abs_reciprocal_sqrt, scale=1.0 / (CLIP * CLIP), bias=1.0
         )
         for part in range(1, len(parts)):
             copy_embedding(part)
@@ -306,17 +307,19 @@ def tile_gep_pa_kernel(tc, target_grad, bases0, bases1, bases2, out_0, out_1):
             store_embedding(group)
 
         mean = keep.tile([P, n_groups * width], F32, name="mean")
-        for part, (group, cols) in enumerate(parts):
-            count = cols.stop - cols.start
+        pieces = [(group, 0, width) for group in range(last)] + [(last, 0, 320), (last, 320, width)]
+        for index, (group, begin, end) in enumerate(pieces):
             mean_acc = bank_pool.tile([P, width], F32, name="mean_acc", tag="bank")
             nc.tensor.matmul(
-                out=mean_acc[:, :count],
+                out=mean_acc[:, : end - begin],
                 lhsT=factor[:, 0:1].to_broadcast([P, P]),
-                rhs=embedding[group][:, cols],
+                rhs=embedding[group][:, begin:end],
                 start=True,
                 stop=True,
             )
-            copy = nc.scalar.copy if part % 2 else nc.vector.tensor_copy
-            start = group * width + cols.start
-            copy(out=mean[:, start : start + count], in_=mean_acc[:, :count])
-        nc.sync.dma_start(out=out_1.rearrange("(o n) -> o n", o=1), in_=mean[0:1, :])
+            out = mean[:, group * width + begin : group * width + end]
+            if index % 2:
+                nc.scalar.mul(out, mean_acc[:, : end - begin], 1.0 / P)
+            else:
+                nc.vector.tensor_scalar_mul(out, mean_acc[:, : end - begin], 1.0 / P)
+        nc.scalar.dma_start(out=out_1.rearrange("(o n) -> o n", o=1), in_=mean[0:1, :])

@@ -21,6 +21,7 @@ SCALAR_COLS = (256, 272, 288, 304)
 MID_COLS = 464
 FIRST_COLS = 192
 LATE = 5
+FACTOR_AT = 2
 CLIP = 1.0
 
 FLOPS = 2 * 128 * 20480 * 512 + 2 * 128 * 1536
@@ -71,7 +72,7 @@ def tile_gep_pa_kernel(tc, target_grad, bases0, bases1, bases2, out_0, out_1):
         sumsq = keep.tile([P, len(parts) + 1], F32, name="sumsq")
         nc.vector.memset(sumsq[:, last_part : last_part + 1], -CLIP * CLIP)
         squares = keep.tile([P, width], F32, name="squares")
-        embedding = [keep.tile([P, width], F32, name="embedding%d" % g) for g in range(n_groups)]
+        embedding = keep.tile([P, n_groups * width], F32, name="embedding")
         acc = [acc_pool.tile([P, width], F32, name="acc%d" % part) for part in range(len(parts))]
 
         chunks = {}
@@ -198,12 +199,15 @@ def tile_gep_pa_kernel(tc, target_grad, bases0, bases1, bases2, out_0, out_1):
                 accum_out=sumsq[:, part + (part == last_part) : part + (part == last_part) + 1],
             )
 
-        def copy_embedding(part):
+        def copy_embedding(part, copy):
             group, cols = parts[part]
-            nc.vector.tensor_copy(out=embedding[group][:, cols], in_=acc[part][:, : cols.stop - cols.start])
+            start = group * width + cols.start
+            count = cols.stop - cols.start
+            copy(out=embedding[:, start : start + count], in_=acc[part][:, :count])
 
         def store_embedding(group):
-            nc.sync.dma_start(out=out_0[:, group * width : (group + 1) * width], in_=embedding[group][:])
+            cols = slice(group * width, (group + 1) * width)
+            nc.sync.dma_start(out=out_0[:, cols], in_=embedding[:, cols])
 
         last = n_groups - 1
         scalar_copy, vector_copy = nc.scalar.copy, nc.vector.tensor_copy
@@ -278,6 +282,7 @@ def tile_gep_pa_kernel(tc, target_grad, bases0, bases1, bases2, out_0, out_1):
             if step - 1 in closed_at:
                 sum_squares(closed_at[step - 1])
 
+        copy_embedding(0, scalar_copy)
         for c, index in enumerate(indices[:-1]):
             if c:
                 keep_clock(1)
@@ -289,37 +294,60 @@ def tile_gep_pa_kernel(tc, target_grad, bases0, bases1, bases2, out_0, out_1):
 
         early = keep.tile([P, 1], F32, name="early")
         sum_squares(last_part - 1)
+        copy_embedding(1, vector_copy)
         nc.vector.tensor_reduce(
             out=early[:], in_=sumsq[:, : last_part + 1], op=ALU.add, axis=mybir.AxisListType.X
         )
         sum_squares(last_part)
-        copy_embedding(0)
-        keep_clock(2)
+        copy_embedding(last_part - 1, vector_copy)
+        copy_embedding(last_part, vector_copy)
+        for group in range(n_groups):
+            store_embedding(group)
+
         excess = keep.tile([P, 1], F32, name="excess")
         nc.scalar.activation(out=excess[:], in_=sumsq[:, last_part + 1 :], func=ACT.Relu, bias=early[:])
         factor = keep.tile([P, 1], F32, name="factor")
         nc.scalar.activation(
             out=factor[:], in_=excess[:], func=ACT.Abs_reciprocal_sqrt, scale=1.0 / (CLIP * CLIP), bias=1.0
         )
-        for part in range(1, len(parts)):
-            copy_embedding(part)
-        for group in range(n_groups):
-            store_embedding(group)
 
-        mean = keep.tile([P, n_groups * width], F32, name="mean")
-        pieces = [(group, 0, width) for group in range(last)] + [(last, 0, 320), (last, 320, width)]
-        for index, (group, begin, end) in enumerate(pieces):
-            mean_acc = bank_pool.tile([P, width], F32, name="mean_acc", tag="bank")
+        early_width = last * width
+        turn = early_width // P
+        every_turn = embedding[:, :early_width].rearrange("b (p i) -> b i p", i=turn)
+        turned = [bank_pool.tile([P, turn // 2, P], F32, name="turned", tag="bank") for unused in range(2)]
+        factor_bank = bank_pool.tile([P, P], F32, name="factor_bank", tag="bank")
+        for i in range(turn):
+            if i == FACTOR_AT:
+                nc.tensor.transpose(factor_bank[:], factor[:, 0:1].to_broadcast([P, P]), identity[:])
+            nc.tensor.transpose(
+                turned[i // (turn // 2)][:, i % (turn // 2), :], every_turn[:, i, :], identity[:]
+            )
+        factor_row = keep.tile([P, P], F32, name="factor_row")
+        nc.scalar.copy(out=factor_row[:], in_=factor_bank[:])
+
+        mean_last = keep.tile([P, width], F32, name="mean_last")
+        for index, cols in enumerate(halves):
+            mean_acc = acc_pool.tile([P, width], F32, name="mean_acc", tag="acc%d" % index)
             nc.tensor.matmul(
-                out=mean_acc[:, : end - begin],
+                out=mean_acc[:, cols],
                 lhsT=factor[:, 0:1].to_broadcast([P, P]),
-                rhs=embedding[group][:, begin:end],
+                rhs=embedding[:, early_width + cols.start : early_width + cols.stop],
                 start=True,
                 stop=True,
             )
-            out = mean[:, group * width + begin : group * width + end]
-            if index % 2:
-                nc.scalar.mul(out, mean_acc[:, : end - begin], 1.0 / P)
-            else:
-                nc.vector.tensor_scalar_mul(out, mean_acc[:, : end - begin], 1.0 / P)
-        nc.scalar.dma_start(out=out_1.rearrange("(o n) -> o n", o=1), in_=mean[0:1, :])
+            nc.scalar.mul(mean_last[:, cols], mean_acc[:, cols], 1.0 / P)
+        nc.scalar.dma_start(out=out_1[early_width:].rearrange("(o n) -> o n", o=1), in_=mean_last[0:1, :])
+
+        products = keep.tile([P, turn, P], F32, name="products")
+        mean_early = keep.tile([P, turn], F32, name="mean_early")
+        for i in range(turn):
+            nc.vector.scalar_tensor_tensor(
+                out=products[:, i, :],
+                in0=turned[i // (turn // 2)][:, i % (turn // 2), :],
+                scalar=1.0 / P,
+                in1=factor_row[:],
+                op0=ALU.mult,
+                op1=ALU.mult,
+                accum_out=mean_early[:, i : i + 1],
+            )
+        nc.sync.dma_start(out=out_1[:early_width].rearrange("(p i) -> p i", i=turn), in_=mean_early[:])

@@ -17,11 +17,10 @@ K_PASS = P * PACK
 QUAD = 4
 SIDES = 2
 LINE = 8
-SCALAR_COLS = (256, 272, 288, 304)
+SCALAR_COLS = (240, 256, 272, 288)
 MID_COLS = 464
 FIRST_COLS = 192
 LATE = 5
-FACTOR_AT = 2
 CLIP = 1.0
 
 FLOPS = 2 * 128 * 20480 * 512 + 2 * 128 * 1536
@@ -282,7 +281,18 @@ def tile_gep_pa_kernel(tc, target_grad, bases0, bases1, bases2, out_0, out_1):
             if step - 1 in closed_at:
                 sum_squares(closed_at[step - 1])
 
-        copy_embedding(0, scalar_copy)
+        early_width = last * width
+        turn = early_width // P
+        blocks = keep.tile([P, turn, P], F32, name="blocks")
+
+        def copy_blocks(group, copy):
+            places = P // last
+            copy(
+                out=blocks[:, :, group * places : (group + 1) * places],
+                in_=acc[group][:].rearrange("b (p i) -> b i p", i=turn),
+            )
+
+        copy_blocks(0, scalar_copy)
         for c, index in enumerate(indices[:-1]):
             if c:
                 keep_clock(1)
@@ -294,48 +304,56 @@ def tile_gep_pa_kernel(tc, target_grad, bases0, bases1, bases2, out_0, out_1):
 
         early = keep.tile([P, 1], F32, name="early")
         sum_squares(last_part - 1)
-        copy_embedding(1, vector_copy)
+        copy_blocks(1, vector_copy)
         nc.vector.tensor_reduce(
             out=early[:], in_=sumsq[:, : last_part + 1], op=ALU.add, axis=mybir.AxisListType.X
         )
         sum_squares(last_part)
         copy_embedding(last_part - 1, vector_copy)
         copy_embedding(last_part, vector_copy)
-        for group in range(n_groups):
-            store_embedding(group)
+        store_embedding(last)
+
+        def clip_factor(out, source):
+            nc.scalar.activation(
+                out=out[:], in_=source[:], func=ACT.Abs_reciprocal_sqrt, scale=1.0 / (CLIP * CLIP), bias=1.0
+            )
 
         excess = keep.tile([P, 1], F32, name="excess")
         nc.scalar.activation(out=excess[:], in_=sumsq[:, last_part + 1 :], func=ACT.Relu, bias=early[:])
         factor = keep.tile([P, 1], F32, name="factor")
-        nc.scalar.activation(
-            out=factor[:], in_=excess[:], func=ACT.Abs_reciprocal_sqrt, scale=1.0 / (CLIP * CLIP), bias=1.0
-        )
+        clip_factor(factor, excess)
 
-        early_width = last * width
-        turn = early_width // P
-        every_turn = embedding[:, :early_width].rearrange("b (p i) -> b i p", i=turn)
+        excess_bank = bank_pool.tile([P, P], F32, name="excess_bank", tag="bank")
         turned = [bank_pool.tile([P, turn // 2, P], F32, name="turned", tag="bank") for unused in range(2)]
-        factor_bank = bank_pool.tile([P, P], F32, name="factor_bank", tag="bank")
-        for i in range(turn):
-            if i == FACTOR_AT:
-                nc.tensor.transpose(factor_bank[:], factor[:, 0:1].to_broadcast([P, P]), identity[:])
-            nc.tensor.transpose(
-                turned[i // (turn // 2)][:, i % (turn // 2), :], every_turn[:, i, :], identity[:]
-            )
-        factor_row = keep.tile([P, P], F32, name="factor_row")
-        nc.scalar.copy(out=factor_row[:], in_=factor_bank[:])
-
         mean_last = keep.tile([P, width], F32, name="mean_last")
-        for index, cols in enumerate(halves):
-            mean_acc = acc_pool.tile([P, width], F32, name="mean_acc", tag="acc%d" % index)
+        mean_acc = []
+
+        def multiply_mean(half):
+            cols = halves[half]
+            mean_acc.append(bank_pool.tile([P, width], F32, name="mean_acc", tag="bank"))
             nc.tensor.matmul(
-                out=mean_acc[:, cols],
+                out=mean_acc[half][:, cols],
                 lhsT=factor[:, 0:1].to_broadcast([P, P]),
                 rhs=embedding[:, early_width + cols.start : early_width + cols.stop],
                 start=True,
                 stop=True,
             )
-            nc.scalar.mul(mean_last[:, cols], mean_acc[:, cols], 1.0 / P)
+
+        factor_row = keep.tile([P, P], F32, name="factor_row")
+        for i in range(turn):
+            nc.tensor.transpose(
+                turned[i // (turn // 2)][:, i % (turn // 2), :], blocks[:, i, :], identity[:]
+            )
+            if i == 0:
+                nc.tensor.transpose(excess_bank[:], excess[:, 0:1].to_broadcast([P, P]), identity[:])
+                clip_factor(factor_row, excess_bank)
+        for half in range(2):
+            multiply_mean(half)
+        for group in range(last):
+            copy_embedding(group, scalar_copy)
+            store_embedding(group)
+        for half, cols in enumerate(halves):
+            nc.scalar.mul(mean_last[:, cols], mean_acc[half][:, cols], 1.0 / P)
         nc.scalar.dma_start(out=out_1[early_width:].rearrange("(o n) -> o n", o=1), in_=mean_last[0:1, :])
 
         products = keep.tile([P, turn, P], F32, name="products")

@@ -18,7 +18,7 @@ QUAD = 4
 SIDES = 2
 LINE = 8
 SCALAR_COLS = (240, 256, 272, 288)
-MID_COLS = 464
+MID_COLS = 416
 FIRST_COLS = 192
 LATE = 5
 CLIP = 1.0
@@ -230,7 +230,7 @@ def tile_gep_pa_kernel(tc, target_grad, bases0, bases1, bases2, out_0, out_1):
                 if step == 1:
                     transpose_grad(1)
                     copy_grad(1)
-                regroup(scalar_copy, indices[3], 0, MID_COLS if step else width)
+                regroup(scalar_copy, indices[3], 0, width if step % 2 else MID_COLS)
             else:
                 for c, index in enumerate(indices):
                     regroup(scalar_copy, index, 0, SCALAR_COLS[c])
@@ -246,12 +246,13 @@ def tile_gep_pa_kernel(tc, target_grad, bases0, bases1, bases2, out_0, out_1):
                 else:
                     quantise(step - 1, 1)
                 regroup(vector_copy, indices[2], 0, width)
-                if step:
+                if step and step % 2 == 0:
                     regroup(vector_copy, indices[3], MID_COLS, width)
                 if step in chunks:
                     quantise_grad(step)
                 if step == 0:
                     quantise(step, 0, 1, 2)
+                    regroup(vector_copy, indices[3], MID_COLS, width)
                 else:
                     quantise(step, 0)
                 if step > 0:
@@ -301,6 +302,7 @@ def tile_gep_pa_kernel(tc, target_grad, bases0, bases1, bases2, out_0, out_1):
             if group == last:
                 quantise_half(indices[-1], cols)
                 multiply(indices[-1], part)
+        keep_clock(1)
 
         early = keep.tile([P, 1], F32, name="early")
         sum_squares(last_part - 1)
@@ -324,13 +326,17 @@ def tile_gep_pa_kernel(tc, target_grad, bases0, bases1, bases2, out_0, out_1):
         clip_factor(factor, excess)
 
         excess_bank = bank_pool.tile([P, P], F32, name="excess_bank", tag="bank")
-        turned = [bank_pool.tile([P, turn // 2, P], F32, name="turned", tag="bank") for unused in range(2)]
+        turned = []
+        for count in (2, 3, 3):
+            bank = bank_pool.tile([P, count, P], F32, name="turned", tag="bank")
+            turned.extend(bank[:, i, :] for i in range(count))
+        assert len(turned) == turn
         mean_last = keep.tile([P, width], F32, name="mean_last")
         mean_acc = []
 
         def multiply_mean(half):
             cols = halves[half]
-            mean_acc.append(bank_pool.tile([P, width], F32, name="mean_acc", tag="bank"))
+            mean_acc.append(acc_pool.tile([P, width], F32, name="mean_acc", tag="acc%d" % (last + half)))
             nc.tensor.matmul(
                 out=mean_acc[half][:, cols],
                 lhsT=factor[:, 0:1].to_broadcast([P, P]),
@@ -342,9 +348,9 @@ def tile_gep_pa_kernel(tc, target_grad, bases0, bases1, bases2, out_0, out_1):
         factor_row = keep.tile([P, P], F32, name="factor_row")
         for i in range(turn):
             nc.tensor.transpose(
-                turned[i // (turn // 2)][:, i % (turn // 2), :], blocks[:, i, :], identity[:]
+                turned[i], blocks[:, i, :], identity[:]
             )
-            if i == 0:
+            if i == 1:
                 nc.tensor.transpose(excess_bank[:], excess[:, 0:1].to_broadcast([P, P]), identity[:])
                 clip_factor(factor_row, excess_bank)
         for half in range(2):
@@ -361,7 +367,7 @@ def tile_gep_pa_kernel(tc, target_grad, bases0, bases1, bases2, out_0, out_1):
         for i in range(turn):
             nc.vector.scalar_tensor_tensor(
                 out=products[:, i, :],
-                in0=turned[i // (turn // 2)][:, i % (turn // 2), :],
+                in0=turned[i],
                 scalar=1.0 / P,
                 in1=factor_row[:],
                 op0=ALU.mult,

from contextlib import ExitStack

import concourse.mybir as mybir
from concourse.masks import make_identity

BF16 = mybir.dt.bfloat16
F32 = mybir.dt.float32
U32 = mybir.dt.uint32
U8 = mybir.dt.uint8
FP8X4 = mybir.dt.float8_e4m3fn_x4
ACT = mybir.ActivationFunctionType
ALU = mybir.AluOpType

P = 128
PACK = 4
K_PASS = P * PACK
QUAD = 4
SIDES = 2
LINE = 8
SCALAR_COLS = (240, 256, 272, 288)
MID_COLS = 416
FIRST_COLS = 192
LATE = 5
CLIP = 1.0

FLOPS = 2 * 128 * 20480 * 512 + 2 * 128 * 1536


def tile_gep_pa_kernel(tc, target_grad, bases0, bases1, bases2, out_0, out_1):
    nc = tc.nc
    bases = (bases0, bases1, bases2)
    n_groups = len(bases)
    width = bases0.shape[1]

    passes = []
    for group, basis in enumerate(bases):
        group_passes = basis.shape[0] // K_PASS
        passes.extend((group, i, group_passes) for i in range(group_passes))
    n_quads = len(passes) // QUAD
    final = n_quads - 1
    assert len(passes) * K_PASS == target_grad.shape[1] and n_quads * QUAD == len(passes)

    grad_step = [quad + (quad < n_quads - LATE) for quad in range(n_quads)]

    with ExitStack() as ctx:
        keep = ctx.enter_context(tc.tile_pool(name="keep", bufs=1))
        grad_pool = ctx.enter_context(tc.tile_pool(name="grad", bufs=2))
        raw_pool = ctx.enter_context(tc.tile_pool(name="raw", bufs=6))
        grouped_pool = ctx.enter_context(tc.tile_pool(name="grouped", bufs=2))
        codes_pool = ctx.enter_context(tc.tile_pool(name="codes", bufs=4))
        acc_pool = ctx.enter_context(tc.psum_pool(name="acc", bufs=1))
        bank_pool = ctx.enter_context(tc.psum_pool(name="bank", bufs=4))
        ctx.enter_context(tc.manual_schedule())

        identity = keep.tile([P, P], F32, name="identity")
        make_identity(nc, identity[:])

        one = keep.tile([P, 1], F32, name="one")
        nc.vector.memset(one[:], 1.0)
        one_root = keep.tile([P, 1], F32, name="one_root")
        nc.scalar.activation(out=one_root[:], in_=one[:], func=ACT.Abs_reciprocal_sqrt)

        zeros = keep.tile([P, width], BF16, name="zeros")
        nc.gpsimd.memset(zeros[:], 0.0)

        grad_codes = keep.tile([P, len(passes) * P], U32, name="grad_codes", align_bytes=64)
        grad_scales = keep.tile([P, len(passes) * P], U8, name="grad_scales", align_bytes=64)
        halves = [slice(0, width // 2), slice(width // 2, width)]
        parts = [(group, slice(0, width)) for group in range(n_groups - 1)] + [(n_groups - 1, cols) for cols in halves]
        last_part = len(parts) - 1
        sumsq = keep.tile([P, len(parts) + 1], F32, name="sumsq")
        nc.vector.memset(sumsq[:, last_part : last_part + 1], -CLIP * CLIP)
        squares = keep.tile([P, width], F32, name="squares")
        embedding = keep.tile([P, n_groups * width], F32, name="embedding")
        acc = [acc_pool.tile([P, width], F32, name="acc%d" % part) for part in range(len(parts))]

        chunks = {}
        for quad in range(n_quads):
            chunks.setdefault(grad_step[quad], []).append(quad)
        grad_raw = {}
        grad_grouped = {}
        flipped = {}

        def load_grad(step):
            columns = QUAD * K_PASS
            grad_raw[step] = grad_pool.tile([P, len(chunks[step]) * columns], BF16, name="grad_raw")
            for index, quad in enumerate(chunks[step]):
                nc.sync.dma_start(
                    out=grad_raw[step][:, index * columns : (index + 1) * columns],
                    in_=target_grad[:, quad * columns : (quad + 1) * columns],
                )

        def transpose_grad(step):
            words = grad_raw[step][:].bitcast(F32).rearrange("b (c p u) -> b c u p", p=P, u=2)
            for index, quad in enumerate(chunks[step]):
                flipped[quad] = []
                for first in (0, 2):
                    bank = bank_pool.tile([P, 2, 2, P], F32, name="bank")
                    for c in range(2):
                        for u in range(2):
                            nc.tensor.transpose(
                                bank[:, c, u, :], words[:, index * QUAD + first + c, u, :], identity[:]
                            )
                    flipped[quad].append(bank)

        def copy_grad(step):
            grad_grouped[step] = grad_pool.tile(
                [P, len(chunks[step]) * QUAD * P * PACK], BF16, name="grad_grouped", align_bytes=64
            )
            words = grad_grouped[step][:].bitcast(F32).rearrange("p (c b u) -> p c b u", b=P, u=2)
            for index, quad in enumerate(chunks[step]):
                for half, bank in enumerate(flipped[quad]):
                    begin = index * QUAD + 2 * half
                    nc.scalar.copy(out=words[:, begin : begin + 2], in_=bank[:].rearrange("p c u b -> p c b u"))

        def quantise_grad(step):
            cols = slice(chunks[step][0] * QUAD * P, (chunks[step][-1] + 1) * QUAD * P)
            nc.vector.quantize_mx(
                out=grad_codes[:, cols].bitcast(FP8X4), scales=grad_scales[:, cols], in_=grad_grouped[step][:]
            )

        raw = {}
        grouped = {}
        codes = {}
        scales = {}

        def load(index):
            group, i, group_passes = passes[index]
            raw[index] = raw_pool.tile([P, PACK, width], BF16, name="raw%d" % (index % SIDES))
            rows = bases[group][i * K_PASS : (i + 1) * K_PASS, :]
            nc.sync.dma_start(out=raw[index][:], in_=rows.rearrange("(p j) n -> p j n", j=PACK))

        def regroup(copy, index, begin, end):
            quad, c = divmod(index, QUAD)
            key = (quad, c % SIDES)
            if key not in grouped:
                grouped[key] = grouped_pool.tile(
                    [P, 2, width, PACK], BF16, name="grouped%d" % key[1], align_bytes=64
                )
            copy(
                out=grouped[key][:, c // SIDES, begin:end].rearrange("p (c i) j -> p c j i", i=LINE),
                in_=raw[index][:, :, begin:end].rearrange("p j (c i) -> p c j i", i=LINE),
            )

        def quantise_half(index, cols):
            quad, c = divmod(index, QUAD)
            key = (quad, c % SIDES)
            base = (c // SIDES) * width
            words = slice(base + cols.start, base + cols.stop)
            nc.vector.quantize_mx(
                out=codes[key][:, words].bitcast(FP8X4),
                scales=scales[key][:, words],
                in_=grouped[key][:, c // SIDES, cols].rearrange("p n j -> p (n j)"),
            )

        def quantise(quad, side, begin=0, end=2):
            key = (quad, side)
            if key not in codes:
                codes[key] = codes_pool.tile([P, 2 * width], U32, name="codes%d" % side, align_bytes=64)
                scales[key] = codes_pool.tile([P, 2 * width], U8, name="scales%d" % side, align_bytes=64)
            cols = slice(begin * width, end * width)
            nc.vector.quantize_mx(
                out=codes[key][:, cols].bitcast(FP8X4),
                scales=scales[key][:, cols],
                in_=grouped[key][:, begin:end].rearrange("p q n j -> p (q n j)"),
            )

        def multiply(index, chosen=None):
            group, i, group_passes = passes[index]
            quad, c = divmod(index, QUAD)
            key = (quad, c % SIDES)
            base = (c // SIDES) * width
            grad_cols = slice(index * P, (index + 1) * P)
            for part, (owner, cols) in enumerate(parts):
                if owner == group and chosen in (None, part):
                    words = slice(base + cols.start, base + cols.stop)
                    nc.tensor.matmul_mx(
                        out=acc[part][:, : cols.stop - cols.start],
                        lhsT=grad_codes[:, grad_cols].bitcast(FP8X4),
                        lhsT_scale=grad_scales[:, grad_cols],
                        rhs=codes[key][:, words].bitcast(FP8X4),
                        rhs_scale=scales[key][:, words],
                        start=(i == 0),
                        stop=(i == group_passes - 1),
                    )

        def keep_clock(count):
            idle_acc = bank_pool.tile([P, width], F32, name="idle_acc", tag="bank")
            for unused in range(count):
                nc.tensor.matmul(out=idle_acc[:], lhsT=zeros[:, :P], rhs=zeros[:], start=True, stop=True)

        def sum_squares(part):
            cols = parts[part][1]
            nc.scalar.activation(
                out=squares[:, cols],
                in_=acc[part][:, : cols.stop - cols.start],
                func=ACT.Square,
                accum_out=sumsq[:, part + (part == last_part) : part + (part == last_part) + 1],
            )

        def copy_embedding(part, copy):
            group, cols = parts[part]
            start = group * width + cols.start
            count = cols.stop - cols.start
            copy(out=embedding[:, start : start + count], in_=acc[part][:, :count])

        def store_embedding(group):
            cols = slice(group * width, (group + 1) * width)
            nc.sync.dma_start(out=out_0[:, cols], in_=embedding[:, cols])

        last = n_groups - 1
        scalar_copy, vector_copy = nc.scalar.copy, nc.vector.tensor_copy
        ready = []
        closed_at = {}
        for step in range(n_quads):
            indices = [step * QUAD + c for c in range(QUAD)]
            for index in indices[:2]:
                load(index)
            if step == 1:
                load_grad(1)
            for index in indices[2:]:
                load(index)
            if step and step + 1 in chunks:
                load_grad(step + 1)

            if step < final:
                if step == 0:
                    regroup(scalar_copy, 0, 0, FIRST_COLS)
                regroup(scalar_copy, indices[1], 0, width)
                if step == 1:
                    transpose_grad(1)
                    copy_grad(1)
                regroup(scalar_copy, indices[3], 0, width if step % 2 else MID_COLS)
            else:
                for c, index in enumerate(indices):
                    regroup(scalar_copy, index, 0, SCALAR_COLS[c])

            if step and step + 1 in chunks:
                transpose_grad(step + 1)
                copy_grad(step + 1)

            if step < final:
                regroup(vector_copy, indices[0], FIRST_COLS if step == 0 else 0, width)
                if step == 0:
                    quantise(step, 0, 0, 1)
                else:
                    quantise(step - 1, 1)
                regroup(vector_copy, indices[2], 0, width)
                if step and step % 2 == 0:
                    regroup(vector_copy, indices[3], MID_COLS, width)
                if step in chunks:
                    quantise_grad(step)
                if step == 0:
                    quantise(step, 0, 1, 2)
                    regroup(vector_copy, indices[3], MID_COLS, width)
                else:
                    quantise(step, 0)
                if step > 0:
                    ready += [(step - 1) * QUAD + c for c in (1, 3)]
                ready += indices[0::2]
                waiting = []
                for index in ready:
                    if grad_step[index // QUAD] <= step:
                        multiply(index)
                        if passes[index][1] == passes[index][2] - 1:
                            closed_at[step] = passes[index][0]
                    else:
                        waiting.append(index)
                ready = waiting
            else:
                for c, index in enumerate(indices):
                    regroup(vector_copy, index, SCALAR_COLS[c], width)
                    if c == 0:
                        quantise(step - 1, 1)
                    else:
                        quantise(step, (c - 1) % SIDES, (c - 1) // SIDES, (c - 1) // SIDES + 1)
                    if c == 1:
                        quantise_grad(step)
                for index in ready + [(step - 1) * QUAD + c for c in (1, 3)]:
                    multiply(index)

            if step - 1 in closed_at:
                sum_squares(closed_at[step - 1])

        early_width = last * width
        turn = early_width // P
        blocks = keep.tile([P, turn, P], F32, name="blocks")

        def copy_blocks(group, copy):
            places = P // last
            copy(
                out=blocks[:, :, group * places : (group + 1) * places],
                in_=acc[group][:].rearrange("b (p i) -> b i p", i=turn),
            )

        copy_blocks(0, scalar_copy)
        for c, index in enumerate(indices[:-1]):
            if c:
                keep_clock(1)
            multiply(index)
        for part, (group, cols) in enumerate(parts):
            if group == last:
                quantise_half(indices[-1], cols)
                multiply(indices[-1], part)
        keep_clock(1)

        early = keep.tile([P, 1], F32, name="early")
        sum_squares(last_part - 1)
        copy_blocks(1, vector_copy)
        nc.vector.tensor_reduce(
            out=early[:], in_=sumsq[:, : last_part + 1], op=ALU.add, axis=mybir.AxisListType.X
        )
        sum_squares(last_part)
        copy_embedding(last_part - 1, vector_copy)
        copy_embedding(last_part, vector_copy)
        store_embedding(last)

        def clip_factor(out, source):
            nc.scalar.activation(
                out=out[:], in_=source[:], func=ACT.Abs_reciprocal_sqrt, scale=1.0 / (CLIP * CLIP), bias=1.0
            )

        excess = keep.tile([P, 1], F32, name="excess")
        nc.scalar.activation(out=excess[:], in_=sumsq[:, last_part + 1 :], func=ACT.Relu, bias=early[:])
        factor = keep.tile([P, 1], F32, name="factor")
        clip_factor(factor, excess)

        excess_bank = bank_pool.tile([P, P], F32, name="excess_bank", tag="bank")
        turned = []
        for count in (2, 3, 3):
            bank = bank_pool.tile([P, count, P], F32, name="turned", tag="bank")
            turned.extend(bank[:, i, :] for i in range(count))
        assert len(turned) == turn
        mean_last = keep.tile([P, width], F32, name="mean_last")
        mean_acc = []

        def multiply_mean(half):
            cols = halves[half]
            mean_acc.append(acc_pool.tile([P, width], F32, name="mean_acc", tag="acc%d" % (last + half)))
            nc.tensor.matmul(
                out=mean_acc[half][:, cols],
                lhsT=factor[:, 0:1].to_broadcast([P, P]),
                rhs=embedding[:, early_width + cols.start : early_width + cols.stop],
                start=True,
                stop=True,
            )

        factor_row = keep.tile([P, P], F32, name="factor_row")
        for i in range(turn):
            nc.tensor.transpose(
                turned[i], blocks[:, i, :], identity[:]
            )
            if i == 1:
                nc.tensor.transpose(excess_bank[:], excess[:, 0:1].to_broadcast([P, P]), identity[:])
                clip_factor(factor_row, excess_bank)
        for half in range(2):
            multiply_mean(half)
        for group in range(last):
            copy_embedding(group, scalar_copy)
            store_embedding(group)
        for half, cols in enumerate(halves):
            nc.scalar.mul(mean_last[:, cols], mean_acc[half][:, cols], 1.0 / P)
        nc.scalar.dma_start(out=out_1[early_width:].rearrange("(o n) -> o n", o=1), in_=mean_last[0:1, :])

        products = keep.tile([P, turn, P], F32, name="products")
        mean_early = keep.tile([P, turn], F32, name="mean_early")
        for i in range(turn):
            nc.vector.scalar_tensor_tensor(
                out=products[:, i, :],
                in0=turned[i],
                scalar=1.0 / P,
                in1=factor_row[:],
                op0=ALU.mult,
                op1=ALU.mult,
                accum_out=mean_early[:, i : i + 1],
            )
        nc.sync.dma_start(out=out_1[:early_width].rearrange("(p i) -> p i", i=turn), in_=mean_early[:])
